import numpy as np
import ml_dtypes


def mxq(x, axis, fmt="e4m3"):
    dtype, down = {"e4m3": (ml_dtypes.float8_e4m3fn, 7), "e5m2": (ml_dtypes.float8_e5m2, 14)}[fmt]
    v = np.moveaxis(np.asarray(x, np.float32).astype(ml_dtypes.bfloat16).astype(np.float64), axis, -1)
    blocks = v.reshape(v.shape[:-1] + (-1, 32))
    amax = np.abs(blocks).max(-1, keepdims=True)
    byte = np.maximum(np.where(amax > 0, np.frexp(amax)[1] - 1 + 127, 0) - down, 1)
    scale = np.exp2(byte - 127.0)
    codes = (blocks / scale).astype(np.float32).astype(dtype).astype(np.float64)
    return np.moveaxis((codes * scale).reshape(v.shape), -1, axis)


WIDE = False


def mx_kscale(k):
    if not WIDE:
        return np.ones(k)
    levels = np.array([10, -10, 5, -5, 0])
    a = np.random.permutation(np.resize(levels, k // 512 * 4)).reshape(k // 512, 4)
    idx = np.arange(k)
    return np.exp2(a[idx // 512, idx % 128 // 32])


BF16 = ml_dtypes.bfloat16


def bf(x):
    return np.asarray(x, np.float32).astype(BF16)


def f64(x):
    return np.asarray(x).astype(np.float64)


E2M1 = np.array([0.0, 0.5, 1.0, 1.5, 2.0, 3.0, 4.0, 6.0, -0.0, -0.5, -1.0, -1.5, -2.0, -3.0, -4.0, -6.0])


def pack_weight(w, fmt):
    k, n = w.shape
    w = f64(bf(w)).reshape(k // 32, 32, n)
    amax = np.abs(w).max(1)
    if fmt == "e4m3":
        byte = np.frexp(amax)[1] - 1 + 127 - 7
    else:
        mant, ex = np.frexp(amax / 6.0)
        byte = np.where(mant > 0.5, ex, ex - 1) + 127
    byte = np.clip(np.where(amax > 0, byte, 1), 1, 254)
    scaled = (w * np.exp2(127.0 - byte)[:, None, :]).reshape(k, n).astype(np.float32)
    by_word = np.ascontiguousarray(scaled.reshape(k // 512, 128, 4, n).transpose(0, 1, 3, 2))
    if fmt == "e4m3":
        words = by_word.astype(ml_dtypes.float8_e4m3fn).view(np.uint8)
    else:
        c = by_word.astype(ml_dtypes.float4_e2m1fn).view(np.uint8) & 0xF
        words = c[..., 0::2] | (c[..., 1::2] << 4)
    return np.ascontiguousarray(words), np.ascontiguousarray(byte.astype(np.uint8).reshape(k // 512, 16, n))


def unpack_weight(words, scales, fmt):
    g, p, n, _ = words.shape
    if fmt == "e4m3":
        vals = np.ascontiguousarray(words).view(ml_dtypes.float8_e4m3fn).astype(np.float64)
    else:
        nib = np.empty((g, p, n, 4), np.uint8)
        nib[..., 0::2] = words & 0xF
        nib[..., 1::2] = words >> 4
        vals = E2M1[nib]
    vals = vals * np.repeat(np.exp2(scales.astype(np.float64) - 127.0), 8, axis=1)[..., None]
    return vals.transpose(0, 1, 3, 2).reshape(g * 512, n)

def pack4(w):
    words, scales = pack_weight(w, "e2m1")
    return words.reshape(words.shape[0], 128, -1), scales


def unpack4(words, scales):
    return unpack_weight(words.reshape(words.shape[0], 128, -1, 2), scales, "e2m1")


B, CIN, CMID, C4, C8, COUT, T, H, W = 4, 512, 1024, 256, 128, 128, 8, 16, 16
S = T * H * W


def setup_inputs():
    s = mx_kscale(CMID)
    h_add = np.maximum(np.random.standard_normal((B, CMID, S)) * np.sqrt(2.0), 0.0)
    h_occ = np.maximum(np.random.standard_normal((B, C8, S)) * np.sqrt(2.0), 0.0)
    w_add2 = np.random.standard_normal((CIN, CMID)) * np.sqrt(2.0 / CMID) / s[None, :]
    words, scales = pack4(np.ascontiguousarray(w_add2.T))
    return {"h_add": bf(h_add * s[None, :, None]),
            "w_add2_words": words,
            "w_add2_scales": scales,
            "b_add2": bf(np.random.standard_normal(CIN) * 0.3),
            "h_occ": bf(h_occ),
            "w_occ3": bf(np.random.standard_normal((COUT, C8)) / np.sqrt(C8))}


def reference(h_add, w_add2_words, w_add2_scales, b_add2, h_occ, w_occ3):
    feat = (unpack4(w_add2_words, w_add2_scales).T @ mxq(f64(h_add), 1, "e4m3")) + f64(b_add2)[None, :, None]
    occ = np.abs(f64(w_occ3) @ f64(h_occ))
    return (mxq(occ, 2, "e4m3") @ mxq(feat, 2, "e4m3").transpose(0, 2, 1)) / S

@@ -1,0 +1,232 @@
+from contextlib import ExitStack
+
+import concourse.mybir as mybir
+from concourse.masks import make_identity
+
+BF16 = mybir.dt.bfloat16
+F32 = mybir.dt.float32
+I32 = mybir.dt.int32
+U32 = mybir.dt.uint32
+U8 = mybir.dt.uint8
+FP8X4 = mybir.dt.float8_e4m3fn_x4
+FP4X4 = mybir.dt.float4_e2m1fn_x4
+
+P = 128
+PACK = 4
+K_PASS = P * PACK
+
+SAMPLES, C_MID, C_IN, C_OCC, MAPS, VOXELS = 4, 1024, 512, 128, 128, 2048
+K_GROUPS = C_MID // K_PASS
+ROUNDS_PER_SAMPLE = VOXELS // K_PASS
+ROUNDS = SAMPLES * ROUNDS_PER_SAMPLE
+C_BLOCKS = C_IN // P
+
+ROUNDS_IN_FLIGHT = 4
+VECTOR_REGROUP_EVERY = 4
+
+FLOPS = 2 * SAMPLES * VOXELS * (C_IN * C_MID + MAPS * C_OCC + MAPS * C_IN)
+
+
+def tile_occurrencepool_pa_t_kernel(
+    tc, h_add, w_add2_words, w_add2_scales, b_add2, h_occ, w_occ3, out
+):
+    nc = tc.nc
+    with ExitStack() as ctx:
+        ctx.enter_context(tc.manual_schedule())
+        consts = ctx.enter_context(tc.tile_pool(name="consts", bufs=1))
+        occ_in = ctx.enter_context(tc.tile_pool(name="occ_in", bufs=SAMPLES))
+        raw_pool = ctx.enter_context(tc.tile_pool(name="raw", bufs=K_GROUPS * ROUNDS_IN_FLIGHT))
+        grouped_pool = ctx.enter_context(tc.tile_pool(name="grouped", bufs=3 * K_GROUPS))
+        work = ctx.enter_context(tc.tile_pool(name="work", bufs=3))
+        feat_psum = ctx.enter_context(tc.psum_pool(name="feat_psum", bufs=C_BLOCKS + 1))
+        occ_psum = ctx.enter_context(tc.psum_pool(name="occ_psum", bufs=2))
+        out_psum = ctx.enter_context(tc.psum_pool(name="out_psum", bufs=1))
+
+        raw, grouped, h_codes, h_scales = {}, {}, {}, {}
+        feat_acc, feat_grouped, feat_codes, feat_scales = {}, {}, {}, {}
+        occ_hidden, occ_acc, occ_grouped, occ_codes, occ_scales = {}, {}, {}, {}, {}
+        out_acc = {}
+
+        def load_round(n):
+            b, r = divmod(n, ROUNDS_PER_SAMPLE)
+            for g in range(K_GROUPS):
+                rows = h_add[b, g * K_PASS : (g + 1) * K_PASS, r * K_PASS : (r + 1) * K_PASS]
+                raw_tile = raw_pool.tile([P, PACK, K_PASS], BF16, name="raw_tile")
+                nc.sync.dma_start(out=raw_tile[:], in_=rows.rearrange("(p j) v -> p j v", j=PACK))
+                raw[(n, g)] = raw_tile
+            if r == 1:
+                hidden = occ_in.tile([P, VOXELS], BF16, name="hidden")
+                nc.sync.dma_start(out=hidden[:], in_=h_occ[b])
+                occ_hidden[b] = hidden
+
+        load_round(0)
+
+        w_words = consts.tile([P, K_GROUPS, 2 * C_IN], U8, name="w_words", align_bytes=64)
+        nc.sync.dma_start(
+            out=w_words[:].bitcast(I32),
+            in_=w_add2_words.bitcast(I32).rearrange("g p n -> p g n"),
+        )
+        w_scales = consts.tile([P, K_GROUPS, C_IN], U8, name="w_scales", align_bytes=64)
+        nc.vector.memset(w_scales[:].bitcast(I32), 0)
+        scale_rows = w_add2_scales.bitcast(I32).rearrange("g (q s) n -> s q g n", s=4)
+        for s in range(4):
+            nc.sync.dma_start(out=w_scales[s:P:32, :, :].bitcast(I32), in_=scale_rows[s])
+
+        ones = consts.tile([P, P], BF16, name="ones")
+        nc.vector.memset(ones[:], 1.0)
+        bias_row = consts.tile([P, C_IN], BF16, name="bias_row")
+        nc.vector.memset(bias_row[:], 0.0)
+        nc.scalar.dma_start(out=bias_row[0:1, :], in_=b_add2.unsqueeze(0))
+        w_occ_rows = consts.tile([MAPS, C_OCC], BF16, name="w_occ_rows")
+        nc.scalar.dma_start(out=w_occ_rows[:], in_=w_occ3)
+        bias_acc = occ_psum.tile([P, C_IN], F32, name="bias_acc", tag="occ_acc")
+        nc.tensor.matmul(out=bias_acc[:], lhsT=ones[:], rhs=bias_row[:], start=True, stop=True)
+        bias = consts.tile([P, C_IN], F32, name="bias")
+        nc.scalar.copy(out=bias[:], in_=bias_acc[:])
+
+        identity = consts.tile([P, P], BF16, name="identity")
+        make_identity(nc, identity[:])
+        w_occ_acc = occ_psum.tile([C_OCC, MAPS], BF16, name="w_occ_acc", tag="occ_acc")
+        nc.tensor.transpose(w_occ_acc[:], w_occ_rows[:], identity[:])
+        w_occ_t = consts.tile([C_OCC, MAPS], BF16, name="w_occ_t")
+        nc.scalar.copy(out=w_occ_t[:], in_=w_occ_acc[:])
+
+        for n in range(1, ROUNDS_IN_FLIGHT):
+            load_round(n)
+
+        def regroup(n, g):
+            tile_out = grouped_pool.tile([P, K_PASS, PACK], BF16, name="grouped", align_bytes=64)
+            dst = tile_out[:].rearrange("p (c i) j -> p c j i", i=4)
+            src = raw[(n, g)][:].rearrange("p j (c i) -> p c j i", i=4)
+            if g == 0 and n % VECTOR_REGROUP_EVERY == 0:
+                nc.vector.tensor_copy(out=dst, in_=src)
+            else:
+                nc.scalar.copy(out=dst, in_=src)
+            grouped[(n, g)] = tile_out
+
+        def quantise_h(n, g):
+            if g == 0:
+                h_codes[n] = work.tile([P, K_GROUPS, K_PASS], U32, name="h_codes", align_bytes=64)
+                h_scales[n] = work.tile([P, K_GROUPS, K_PASS], U8, name="h_scales", align_bytes=64)
+            nc.vector.quantize_mx(
+                out=h_codes[n][:, g, :].bitcast(FP8X4),
+                scales=h_scales[n][:, g, :],
+                in_=grouped[(n, g)][:].rearrange("p v j -> p (v j)"),
+            )
+
+        def first_product(n, cb):
+            acc = feat_psum.tile([P, PACK, P], F32, name="feat_acc")
+            for t in range(PACK):
+                voxels = slice(t * P, (t + 1) * P)
+                for g in range(K_GROUPS):
+                    nc.tensor.matmul_mx(
+                        out=acc[:, t, :],
+                        lhsT=h_codes[n][:, g, voxels].bitcast(FP8X4),
+                        lhsT_scale=h_scales[n][:, g, voxels],
+                        rhs=w_words[:, g, 2 * P * cb : 2 * P * (cb + 1)].bitcast(FP4X4),
+                        rhs_scale=w_scales[:, g, P * cb : P * (cb + 1)],
+                        start=(g == 0),
+                        stop=(g == K_GROUPS - 1),
+                    )
+            feat_acc[(n, cb)] = acc
+
+        def add_bias(n, cb):
+            if cb == 0:
+                feat_grouped[n] = work.tile(
+                    [P, C_IN, PACK], BF16, name="feat_grouped", align_bytes=64
+                )
+            channels = slice(cb * P, (cb + 1) * P)
+            nc.vector.tensor_tensor(
+                out=feat_grouped[n][:, channels, :],
+                in0=feat_acc[(n, cb)][:].rearrange("p t c -> p c t"),
+                in1=bias[:, channels].unsqueeze(2).to_broadcast([P, P, PACK]),
+                op=mybir.AluOpType.add,
+            )
+
+        def quantise_feat(n):
+            feat_codes[n] = work.tile([P, C_IN], U32, name="feat_codes", align_bytes=64)
+            feat_scales[n] = work.tile([P, C_IN], U8, name="feat_scales", align_bytes=64)
+            nc.vector.quantize_mx(
+                out=feat_codes[n][:].bitcast(FP8X4),
+                scales=feat_scales[n][:],
+                in_=feat_grouped[n][:].rearrange("p c t -> p (c t)"),
+            )
+
+        def occurrence(n):
+            b, r = divmod(n, ROUNDS_PER_SAMPLE)
+            acc = occ_psum.tile([P, PACK, MAPS], F32, name="occ_acc")
+            for t in range(PACK):
+                first = r * K_PASS + t * P
+                nc.tensor.matmul(
+                    out=acc[:, t, :],
+                    lhsT=occ_hidden[b][:, first : first + P],
+                    rhs=w_occ_t[:],
+                    start=True,
+                    stop=True,
+                )
+            occ_grouped[n] = work.tile([P, MAPS, PACK], BF16, name="occ_grouped", align_bytes=64)
+            nc.scalar.activation(
+                out=occ_grouped[n][:],
+                in_=acc[:].rearrange("p t o -> p o t"),
+                func=mybir.ActivationFunctionType.Abs,
+            )
+
+        def quantise_occ(n):
+            occ_codes[n] = work.tile([P, MAPS], U32, name="occ_codes", align_bytes=64)
+            occ_scales[n] = work.tile([P, MAPS], U8, name="occ_scales", align_bytes=64)
+            nc.vector.quantize_mx(
+                out=occ_codes[n][:].bitcast(FP8X4),
+                scales=occ_scales[n][:],
+                in_=occ_grouped[n][:].rearrange("p o t -> p (o t)"),
+            )
+
+        def second_product(n):
+            b, r = divmod(n, ROUNDS_PER_SAMPLE)
+            if r == 0:
+                out_acc[b] = out_psum.tile([MAPS, C_IN], F32, name="out_acc")
+            nc.tensor.matmul_mx(
+                out=out_acc[b][:],
+                lhsT=occ_codes[n][:].bitcast(FP8X4),
+                lhsT_scale=occ_scales[n][:],
+                rhs=feat_codes[n][:].bitcast(FP8X4),
+                rhs_scale=feat_scales[n][:],
+                start=(r == 0),
+                stop=(r == ROUNDS_PER_SAMPLE - 1),
+            )
+
+        def store_sample(b):
+            mean = work.tile([MAPS, C_IN], F32, name="mean")
+            nc.scalar.mul(out=mean[:], in_=out_acc[b][:], mul=1.0 / VOXELS)
+            nc.sync.dma_start(out=out[b], in_=mean[:])
+
+        def exists(n):
+            return 0 <= n < ROUNDS
+
+        for n in range(-2, ROUNDS + 1):
+            if exists(n):
+                add_bias(n, 0)
+            if exists(n - 1):
+                quantise_feat(n - 1)
+                second_product(n - 1)
+            if exists(n):
+                add_bias(n, 1)
+            if exists(n + 1):
+                for g in range(K_GROUPS):
+                    quantise_h(n + 1, g)
+                for cb in range(C_BLOCKS - 1):
+                    first_product(n + 1, cb)
+            if exists(n + 2):
+                for g in range(K_GROUPS):
+                    regroup(n + 2, g)
+            if exists(n + 2 + ROUNDS_IN_FLIGHT):
+                load_round(n + 2 + ROUNDS_IN_FLIGHT)
+            if exists(n):
+                add_bias(n, 2)
+            if exists(n + 1):
+                first_product(n + 1, C_BLOCKS - 1)
+                occurrence(n + 1)
+            if exists(n):
+                add_bias(n, 3)
+                quantise_occ(n)
+            if exists(n - 1) and n % ROUNDS_PER_SAMPLE == 0:
+                store_sample((n - 1) // ROUNDS_PER_SAMPLE)

@@ -22,7 +22,7 @@ ROUNDS = SAMPLES * ROUNDS_PER_SAMPLE
 C_BLOCKS = C_IN // P
 
 ROUNDS_IN_FLIGHT = 4
-VECTOR_REGROUP_EVERY = 4
+VECTOR_VOXELS = 64
 
 FLOPS = 2 * SAMPLES * VOXELS * (C_IN * C_MID + MAPS * C_OCC + MAPS * C_IN)
 
@@ -34,9 +34,8 @@ def tile_occurrencepool_pa_t_kernel(
     with ExitStack() as ctx:
         ctx.enter_context(tc.manual_schedule())
         consts = ctx.enter_context(tc.tile_pool(name="consts", bufs=1))
-        occ_in = ctx.enter_context(tc.tile_pool(name="occ_in", bufs=SAMPLES))
+        occ_in = ctx.enter_context(tc.tile_pool(name="occ_in", bufs=ROUNDS_IN_FLIGHT))
         raw_pool = ctx.enter_context(tc.tile_pool(name="raw", bufs=K_GROUPS * ROUNDS_IN_FLIGHT))
-        grouped_pool = ctx.enter_context(tc.tile_pool(name="grouped", bufs=3 * K_GROUPS))
         work = ctx.enter_context(tc.tile_pool(name="work", bufs=3))
         feat_psum = ctx.enter_context(tc.psum_pool(name="feat_psum", bufs=C_BLOCKS + 1))
         occ_psum = ctx.enter_context(tc.psum_pool(name="occ_psum", bufs=2))
@@ -49,15 +48,15 @@ def tile_occurrencepool_pa_t_kernel(
 
         def load_round(n):
             b, r = divmod(n, ROUNDS_PER_SAMPLE)
+            voxels = slice(r * K_PASS, (r + 1) * K_PASS)
             for g in range(K_GROUPS):
-                rows = h_add[b, g * K_PASS : (g + 1) * K_PASS, r * K_PASS : (r + 1) * K_PASS]
+                rows = h_add[b, g * K_PASS : (g + 1) * K_PASS, voxels]
                 raw_tile = raw_pool.tile([P, PACK, K_PASS], BF16, name="raw_tile")
                 nc.sync.dma_start(out=raw_tile[:], in_=rows.rearrange("(p j) v -> p j v", j=PACK))
                 raw[(n, g)] = raw_tile
-            if r == 1:
-                hidden = occ_in.tile([P, VOXELS], BF16, name="hidden")
-                nc.sync.dma_start(out=hidden[:], in_=h_occ[b])
-                occ_hidden[b] = hidden
+            hidden = occ_in.tile([C_OCC, K_PASS], BF16, name="hidden")
+            nc.sync.dma_start(out=hidden[:], in_=h_occ[b, :, voxels])
+            occ_hidden[n] = hidden
 
         load_round(0)
 
@@ -94,24 +93,32 @@ def tile_occurrencepool_pa_t_kernel(
         for n in range(1, ROUNDS_IN_FLIGHT):
             load_round(n)
 
-        def regroup(n, g):
-            tile_out = grouped_pool.tile([P, K_PASS, PACK], BF16, name="grouped", align_bytes=64)
-            dst = tile_out[:].rearrange("p (c i) j -> p c j i", i=4)
-            src = raw[(n, g)][:].rearrange("p j (c i) -> p c j i", i=4)
-            if g == 0 and n % VECTOR_REGROUP_EVERY == 0:
-                nc.vector.tensor_copy(out=dst, in_=src)
-            else:
-                nc.scalar.copy(out=dst, in_=src)
-            grouped[(n, g)] = tile_out
+        def regroup(n):
+            grouped[n] = work.tile(
+                [P, K_GROUPS, K_PASS, PACK], BF16, name="grouped", align_bytes=64
+            )
+            for g in range(K_GROUPS):
+                dst = grouped[n][:, g, :, :].rearrange("p (c i) j -> p c j i", i=4)
+                src = raw[(n, g)][:].rearrange("p j (c i) -> p c j i", i=4)
+                if n == 0:
+                    vector_voxels = K_PASS
+                elif g == K_GROUPS - 1:
+                    vector_voxels = VECTOR_VOXELS
+                else:
+                    vector_voxels = 0
+                split = (K_PASS - vector_voxels) // 4
+                if split > 0:
+                    nc.scalar.copy(out=dst[:, :split], in_=src[:, :split])
+                if vector_voxels > 0:
+                    nc.vector.tensor_copy(out=dst[:, split:], in_=src[:, split:])
 
-        def quantise_h(n, g):
-            if g == 0:
-                h_codes[n] = work.tile([P, K_GROUPS, K_PASS], U32, name="h_codes", align_bytes=64)
-                h_scales[n] = work.tile([P, K_GROUPS, K_PASS], U8, name="h_scales", align_bytes=64)
+        def quantise_h(n):
+            h_codes[n] = work.tile([P, K_GROUPS, K_PASS], U32, name="h_codes", align_bytes=64)
+            h_scales[n] = work.tile([P, K_GROUPS, K_PASS], U8, name="h_scales", align_bytes=64)
             nc.vector.quantize_mx(
-                out=h_codes[n][:, g, :].bitcast(FP8X4),
-                scales=h_scales[n][:, g, :],
-                in_=grouped[(n, g)][:].rearrange("p v j -> p (v j)"),
+                out=h_codes[n][:].rearrange("p g v -> p (g v)").bitcast(FP8X4),
+                scales=h_scales[n][:].rearrange("p g v -> p (g v)"),
+                in_=grouped[n][:].rearrange("p g v j -> p (g v j)"),
             )
 
         def first_product(n, cb):
@@ -152,22 +159,23 @@ def tile_occurrencepool_pa_t_kernel(
                 in_=feat_grouped[n][:].rearrange("p c t -> p (c t)"),
             )
 
-        def occurrence(n):
-            b, r = divmod(n, ROUNDS_PER_SAMPLE)
+        def occ_product(n):
             acc = occ_psum.tile([P, PACK, MAPS], F32, name="occ_acc")
             for t in range(PACK):
-                first = r * K_PASS + t * P
                 nc.tensor.matmul(
                     out=acc[:, t, :],
-                    lhsT=occ_hidden[b][:, first : first + P],
+                    lhsT=occ_hidden[n][:, t * P : (t + 1) * P],
                     rhs=w_occ_t[:],
                     start=True,
                     stop=True,
                 )
+            occ_acc[n] = acc
+
+        def occ_abs(n):
             occ_grouped[n] = work.tile([P, MAPS, PACK], BF16, name="occ_grouped", align_bytes=64)
             nc.scalar.activation(
                 out=occ_grouped[n][:],
-                in_=acc[:].rearrange("p t o -> p o t"),
+                in_=occ_acc[n][:].rearrange("p t o -> p o t"),
                 func=mybir.ActivationFunctionType.Abs,
             )
 
@@ -211,22 +219,23 @@ def tile_occurrencepool_pa_t_kernel(
             if exists(n):
                 add_bias(n, 1)
             if exists(n + 1):
-                for g in range(K_GROUPS):
-                    quantise_h(n + 1, g)
+                quantise_h(n + 1)
                 for cb in range(C_BLOCKS - 1):
                     first_product(n + 1, cb)
             if exists(n + 2):
-                for g in range(K_GROUPS):
-                    regroup(n + 2, g)
-            if exists(n + 2 + ROUNDS_IN_FLIGHT):
-                load_round(n + 2 + ROUNDS_IN_FLIGHT)
+                regroup(n + 2)
+            if exists(n + 1):
+                occ_abs(n + 1)
             if exists(n):
                 add_bias(n, 2)
             if exists(n + 1):
                 first_product(n + 1, C_BLOCKS - 1)
-                occurrence(n + 1)
+            if exists(n + 2):
+                occ_product(n + 2)
             if exists(n):
                 add_bias(n, 3)
                 quantise_occ(n)
             if exists(n - 1) and n % ROUNDS_PER_SAMPLE == 0:
                 store_sample((n - 1) // ROUNDS_PER_SAMPLE)
+            if exists(n + 2 + ROUNDS_IN_FLIGHT):
+                load_round(n + 2 + ROUNDS_IN_FLIGHT)

@@ -211,29 +211,23 @@ def tile_occurrencepool_pa_t_kernel(
             return 0 <= n < ROUNDS
 
         for n in range(-2, ROUNDS + 1):
-            if exists(n):
-                add_bias(n, 0)
             if exists(n - 1):
                 quantise_feat(n - 1)
                 second_product(n - 1)
-            if exists(n):
-                add_bias(n, 1)
             if exists(n + 1):
                 quantise_h(n + 1)
-                for cb in range(C_BLOCKS - 1):
+            for cb in range(C_BLOCKS):
+                if exists(n + 1):
                     first_product(n + 1, cb)
+                if exists(n):
+                    add_bias(n, cb)
             if exists(n + 2):
                 regroup(n + 2)
             if exists(n + 1):
                 occ_abs(n + 1)
-            if exists(n):
-                add_bias(n, 2)
-            if exists(n + 1):
-                first_product(n + 1, C_BLOCKS - 1)
             if exists(n + 2):
                 occ_product(n + 2)
             if exists(n):
-                add_bias(n, 3)
                 quantise_occ(n)
             if exists(n - 1) and n % ROUNDS_PER_SAMPLE == 0:
                 store_sample((n - 1) // ROUNDS_PER_SAMPLE)

@@ -22,7 +22,7 @@ ROUNDS = SAMPLES * ROUNDS_PER_SAMPLE
 C_BLOCKS = C_IN // P
 
 ROUNDS_IN_FLIGHT = 4
-VECTOR_VOXELS = 64
+VECTOR_VOXELS = 96
 
 FLOPS = 2 * SAMPLES * VOXELS * (C_IN * C_MID + MAPS * C_OCC + MAPS * C_IN)
 
@@ -46,19 +46,35 @@ def tile_occurrencepool_pa_t_kernel(
         occ_hidden, occ_acc, occ_grouped, occ_codes, occ_scales = {}, {}, {}, {}, {}
         out_acc = {}
 
-        def load_round(n):
+        def load_h(n, g):
             b, r = divmod(n, ROUNDS_PER_SAMPLE)
-            voxels = slice(r * K_PASS, (r + 1) * K_PASS)
-            for g in range(K_GROUPS):
-                rows = h_add[b, g * K_PASS : (g + 1) * K_PASS, voxels]
-                raw_tile = raw_pool.tile([P, PACK, K_PASS], BF16, name="raw_tile")
-                nc.sync.dma_start(out=raw_tile[:], in_=rows.rearrange("(p j) v -> p j v", j=PACK))
-                raw[(n, g)] = raw_tile
-            hidden = occ_in.tile([C_OCC, K_PASS], BF16, name="hidden")
-            nc.sync.dma_start(out=hidden[:], in_=h_occ[b, :, voxels])
-            occ_hidden[n] = hidden
+            rows = h_add[b, g * K_PASS : (g + 1) * K_PASS, r * K_PASS : (r + 1) * K_PASS]
+            raw[(n, g)] = raw_pool.tile([P, PACK, K_PASS], BF16, name="raw")
+            nc.sync.dma_start(out=raw[(n, g)][:], in_=rows.rearrange("(p j) v -> p j v", j=PACK))
 
-        load_round(0)
+        def load_hidden(n):
+            b, r = divmod(n, ROUNDS_PER_SAMPLE)
+            occ_hidden[n] = occ_in.tile([C_OCC, K_PASS], BF16, name="hidden")
+            nc.sync.dma_start(
+                out=occ_hidden[n][:], in_=h_occ[b, :, r * K_PASS : (r + 1) * K_PASS]
+            )
+
+        def load_round(n):
+            for g in range(K_GROUPS):
+                load_h(n, g)
+            load_hidden(n)
+
+        w_occ_rows = consts.tile([MAPS, C_OCC], BF16, name="w_occ_rows")
+        nc.sync.dma_start(out=w_occ_rows[:], in_=w_occ3)
+        bias_row = consts.tile([P, C_IN], BF16, name="bias_row")
+        nc.vector.memset(bias_row[:], 0.0)
+        nc.sync.dma_start(out=bias_row[0:1, :], in_=b_add2.unsqueeze(0))
+        ones = consts.tile([P, P], BF16, name="ones")
+        nc.vector.memset(ones[:], 1.0)
+
+        load_h(0, 0)
+        load_h(0, 1)
+        load_h(1, 0)
 
         w_words = consts.tile([P, K_GROUPS, 2 * C_IN], U8, name="w_words", align_bytes=64)
         nc.sync.dma_start(
@@ -71,27 +87,28 @@ def tile_occurrencepool_pa_t_kernel(
         for s in range(4):
             nc.sync.dma_start(out=w_scales[s:P:32, :, :].bitcast(I32), in_=scale_rows[s])
 
-        ones = consts.tile([P, P], BF16, name="ones")
-        nc.vector.memset(ones[:], 1.0)
-        bias_row = consts.tile([P, C_IN], BF16, name="bias_row")
-        nc.vector.memset(bias_row[:], 0.0)
-        nc.scalar.dma_start(out=bias_row[0:1, :], in_=b_add2.unsqueeze(0))
-        w_occ_rows = consts.tile([MAPS, C_OCC], BF16, name="w_occ_rows")
-        nc.scalar.dma_start(out=w_occ_rows[:], in_=w_occ3)
+        load_hidden(0)
+        load_h(1, 1)
+        load_hidden(1)
+        for n in range(2, ROUNDS_IN_FLIGHT):
+            load_round(n)
+
+        warm = consts.tile([P, 1], F32, name="warm")
+        nc.scalar.activation(
+            out=warm[:], in_=ones[:, 0:1], func=mybir.ActivationFunctionType.Abs
+        )
+
         bias_acc = occ_psum.tile([P, C_IN], F32, name="bias_acc", tag="occ_acc")
         nc.tensor.matmul(out=bias_acc[:], lhsT=ones[:], rhs=bias_row[:], start=True, stop=True)
         bias = consts.tile([P, C_IN], F32, name="bias")
-        nc.scalar.copy(out=bias[:], in_=bias_acc[:])
+        nc.vector.tensor_copy(out=bias[:], in_=bias_acc[:])
 
         identity = consts.tile([P, P], BF16, name="identity")
         make_identity(nc, identity[:])
         w_occ_acc = occ_psum.tile([C_OCC, MAPS], BF16, name="w_occ_acc", tag="occ_acc")
         nc.tensor.transpose(w_occ_acc[:], w_occ_rows[:], identity[:])
         w_occ_t = consts.tile([C_OCC, MAPS], BF16, name="w_occ_t")
-        nc.scalar.copy(out=w_occ_t[:], in_=w_occ_acc[:])
-
-        for n in range(1, ROUNDS_IN_FLIGHT):
-            load_round(n)
+        nc.vector.tensor_copy(out=w_occ_t[:], in_=w_occ_acc[:])
 
         def regroup(n):
             grouped[n] = work.tile(
@@ -100,12 +117,12 @@ def tile_occurrencepool_pa_t_kernel(
             for g in range(K_GROUPS):
                 dst = grouped[n][:, g, :, :].rearrange("p (c i) j -> p c j i", i=4)
                 src = raw[(n, g)][:].rearrange("p j (c i) -> p c j i", i=4)
-                if n == 0:
-                    vector_voxels = K_PASS
-                elif g == K_GROUPS - 1:
-                    vector_voxels = VECTOR_VOXELS
-                else:
+                if g < K_GROUPS - 1:
                     vector_voxels = 0
+                elif n == 0:
+                    vector_voxels = K_PASS
+                else:
+                    vector_voxels = VECTOR_VOXELS
                 split = (K_PASS - vector_voxels) // 4
                 if split > 0:
                     nc.scalar.copy(out=dst[:, :split], in_=src[:, :split])
@@ -211,23 +228,29 @@ def tile_occurrencepool_pa_t_kernel(
             return 0 <= n < ROUNDS
 
         for n in range(-2, ROUNDS + 1):
+            if exists(n):
+                add_bias(n, 0)
             if exists(n - 1):
                 quantise_feat(n - 1)
                 second_product(n - 1)
+            if exists(n):
+                add_bias(n, 1)
             if exists(n + 1):
                 quantise_h(n + 1)
-            for cb in range(C_BLOCKS):
-                if exists(n + 1):
+                for cb in range(C_BLOCKS - 1):
                     first_product(n + 1, cb)
-                if exists(n):
-                    add_bias(n, cb)
             if exists(n + 2):
                 regroup(n + 2)
             if exists(n + 1):
                 occ_abs(n + 1)
+            if exists(n):
+                add_bias(n, 2)
+            if exists(n + 1):
+                first_product(n + 1, C_BLOCKS - 1)
             if exists(n + 2):
                 occ_product(n + 2)
             if exists(n):
+                add_bias(n, 3)
                 quantise_occ(n)
             if exists(n - 1) and n % ROUNDS_PER_SAMPLE == 0:
                 store_sample((n - 1) // ROUNDS_PER_SAMPLE)

@@ -119,10 +119,8 @@ def tile_occurrencepool_pa_t_kernel(
                 src = raw[(n, g)][:].rearrange("p j (c i) -> p c j i", i=4)
                 if g < K_GROUPS - 1:
                     vector_voxels = 0
-                elif n == 0:
-                    vector_voxels = K_PASS
                 else:
-                    vector_voxels = VECTOR_VOXELS
+                    vector_voxels = max(VECTOR_VOXELS, K_PASS >> n)
                 split = (K_PASS - vector_voxels) // 4
                 if split > 0:
                     nc.scalar.copy(out=dst[:, :split], in_=src[:, :split])

@@ -22,7 +22,8 @@ ROUNDS = SAMPLES * ROUNDS_PER_SAMPLE
 C_BLOCKS = C_IN // P
 
 ROUNDS_IN_FLIGHT = 4
-VECTOR_VOXELS = 96
+GPSIMD_VOXELS = 320
+HEAD_ROUNDS = 2
 
 FLOPS = 2 * SAMPLES * VOXELS * (C_IN * C_MID + MAPS * C_OCC + MAPS * C_IN)
 
@@ -37,6 +38,7 @@ def tile_occurrencepool_pa_t_kernel(
         occ_in = ctx.enter_context(tc.tile_pool(name="occ_in", bufs=ROUNDS_IN_FLIGHT))
         raw_pool = ctx.enter_context(tc.tile_pool(name="raw", bufs=K_GROUPS * ROUNDS_IN_FLIGHT))
         work = ctx.enter_context(tc.tile_pool(name="work", bufs=3))
+        grouped_pool = ctx.enter_context(tc.tile_pool(name="grouped_pool", bufs=2))
         feat_psum = ctx.enter_context(tc.psum_pool(name="feat_psum", bufs=C_BLOCKS + 1))
         occ_psum = ctx.enter_context(tc.psum_pool(name="occ_psum", bufs=2))
         out_psum = ctx.enter_context(tc.psum_pool(name="out_psum", bufs=1))
@@ -111,21 +113,33 @@ def tile_occurrencepool_pa_t_kernel(
         nc.vector.tensor_copy(out=w_occ_t[:], in_=w_occ_acc[:])
 
         def regroup(n):
-            grouped[n] = work.tile(
+            grouped[n] = grouped_pool.tile(
                 [P, K_GROUPS, K_PASS, PACK], BF16, name="grouped", align_bytes=64
             )
             for g in range(K_GROUPS):
                 dst = grouped[n][:, g, :, :].rearrange("p (c i) j -> p c j i", i=4)
                 src = raw[(n, g)][:].rearrange("p j (c i) -> p c j i", i=4)
                 if g < K_GROUPS - 1:
-                    vector_voxels = 0
+                    other_voxels = 0
+                elif n < HEAD_ROUNDS:
+                    other_voxels = K_PASS >> n
                 else:
-                    vector_voxels = max(VECTOR_VOXELS, K_PASS >> n)
-                split = (K_PASS - vector_voxels) // 4
+                    other_voxels = GPSIMD_VOXELS
+                first = K_PASS - other_voxels
+                split = first // 4
                 if split > 0:
                     nc.scalar.copy(out=dst[:, :split], in_=src[:, :split])
-                if vector_voxels > 0:
+                if other_voxels > 0 and n < HEAD_ROUNDS:
                     nc.vector.tensor_copy(out=dst[:, split:], in_=src[:, split:])
+                elif other_voxels > 0:
+                    nc.gpsimd.tensor_scalar(
+                        out=grouped[n][:, g, first:, :],
+                        in0=raw[(n, g)][:, :, first:].rearrange("p j v -> p v j"),
+                        scalar1=1.0,
+                        scalar2=0.0,
+                        op0=mybir.AluOpType.mult,
+                        op1=mybir.AluOpType.add,
+                    )
 
         def quantise_h(n):
             h_codes[n] = work.tile([P, K_GROUPS, K_PASS], U32, name="h_codes", align_bytes=64)
@@ -225,32 +239,26 @@ def tile_occurrencepool_pa_t_kernel(
         def exists(n):
             return 0 <= n < ROUNDS
 
-        for n in range(-2, ROUNDS + 1):
-            if exists(n):
-                add_bias(n, 0)
-            if exists(n - 1):
-                quantise_feat(n - 1)
-                second_product(n - 1)
-            if exists(n):
-                add_bias(n, 1)
+        for n in range(-2, ROUNDS):
             if exists(n + 1):
                 quantise_h(n + 1)
-                for cb in range(C_BLOCKS - 1):
-                    first_product(n + 1, cb)
+                first_product(n + 1, 0)
             if exists(n + 2):
                 regroup(n + 2)
             if exists(n + 1):
                 occ_abs(n + 1)
-            if exists(n):
-                add_bias(n, 2)
-            if exists(n + 1):
-                first_product(n + 1, C_BLOCKS - 1)
+            for cb in range(C_BLOCKS):
+                if exists(n):
+                    add_bias(n, cb)
+                if exists(n + 1) and cb + 1 < C_BLOCKS:
+                    first_product(n + 1, cb + 1)
             if exists(n + 2):
                 occ_product(n + 2)
             if exists(n):
-                add_bias(n, 3)
                 quantise_occ(n)
-            if exists(n - 1) and n % ROUNDS_PER_SAMPLE == 0:
-                store_sample((n - 1) // ROUNDS_PER_SAMPLE)
+                quantise_feat(n)
+                second_product(n)
+            if exists(n) and (n + 1) % ROUNDS_PER_SAMPLE == 0:
+                store_sample(n // ROUNDS_PER_SAMPLE)
             if exists(n + 2 + ROUNDS_IN_FLIGHT):
                 load_round(n + 2 + ROUNDS_IN_FLIGHT)

@@ -23,7 +23,8 @@ C_BLOCKS = C_IN // P
 
 ROUNDS_IN_FLIGHT = 4
 GPSIMD_VOXELS = 320
-HEAD_ROUNDS = 2
+SCALAR_VOXELS_0 = 192
+WARM_UP = (4, 2)
 
 FLOPS = 2 * SAMPLES * VOXELS * (C_IN * C_MID + MAPS * C_OCC + MAPS * C_IN)
 
@@ -112,6 +113,17 @@ def tile_occurrencepool_pa_t_kernel(
         w_occ_t = consts.tile([C_OCC, MAPS], BF16, name="w_occ_t")
         nc.vector.tensor_copy(out=w_occ_t[:], in_=w_occ_acc[:])
 
+        warm_acc = feat_psum.tile([P, PACK, P], F32, name="feat_acc")
+        for g in range(K_GROUPS):
+            for j in range(WARM_UP[g]):
+                nc.tensor.matmul(
+                    out=warm_acc[:].rearrange("p t c -> p (t c)"),
+                    lhsT=ones[:],
+                    rhs=raw[(0, g)][:, j, :],
+                    start=True,
+                    stop=True,
+                )
+
         def regroup(n):
             grouped[n] = grouped_pool.tile(
                 [P, K_GROUPS, K_PASS, PACK], BF16, name="grouped", align_bytes=64
@@ -119,19 +131,17 @@ def tile_occurrencepool_pa_t_kernel(
             for g in range(K_GROUPS):
                 dst = grouped[n][:, g, :, :].rearrange("p (c i) j -> p c j i", i=4)
                 src = raw[(n, g)][:].rearrange("p j (c i) -> p c j i", i=4)
-                if g < K_GROUPS - 1:
-                    other_voxels = 0
-                elif n < HEAD_ROUNDS:
-                    other_voxels = K_PASS >> n
+                if n == 0:
+                    first = SCALAR_VOXELS_0
+                elif g < K_GROUPS - 1:
+                    first = K_PASS
                 else:
-                    other_voxels = GPSIMD_VOXELS
-                first = K_PASS - other_voxels
+                    first = K_PASS - GPSIMD_VOXELS
                 split = first // 4
-                if split > 0:
-                    nc.scalar.copy(out=dst[:, :split], in_=src[:, :split])
-                if other_voxels > 0 and n < HEAD_ROUNDS:
+                nc.scalar.copy(out=dst[:, :split], in_=src[:, :split])
+                if n == 0:
                     nc.vector.tensor_copy(out=dst[:, split:], in_=src[:, split:])
-                elif other_voxels > 0:
+                elif first < K_PASS:
                     nc.gpsimd.tensor_scalar(
                         out=grouped[n][:, g, first:, :],
                         in0=raw[(n, g)][:, :, first:].rearrange("p j v -> p v j"),
@@ -240,20 +250,23 @@ def tile_occurrencepool_pa_t_kernel(
             return 0 <= n < ROUNDS
 
         for n in range(-2, ROUNDS):
+            lead = 2 if n == 0 else 0
+            for cb in range(lead):
+                add_bias(n, cb)
             if exists(n + 1):
                 quantise_h(n + 1)
-                first_product(n + 1, 0)
+                for cb in range(lead + 1):
+                    first_product(n + 1, cb)
+                occ_product(n + 1)
             if exists(n + 2):
                 regroup(n + 2)
             if exists(n + 1):
                 occ_abs(n + 1)
-            for cb in range(C_BLOCKS):
+            for cb in range(lead, C_BLOCKS):
                 if exists(n):
                     add_bias(n, cb)
                 if exists(n + 1) and cb + 1 < C_BLOCKS:
                     first_product(n + 1, cb + 1)
-            if exists(n + 2):
-                occ_product(n + 2)
             if exists(n):
                 quantise_occ(n)
                 quantise_feat(n)

@@ -25,6 +25,8 @@ ROUNDS_IN_FLIGHT = 4
 GPSIMD_VOXELS = 320
 SCALAR_VOXELS_0 = 192
 WARM_UP = (4, 2)
+TAIL_ROUNDS = 2
+SCALAR_BLOCKS = 2
 
 FLOPS = 2 * SAMPLES * VOXELS * (C_IN * C_MID + MAPS * C_OCC + MAPS * C_IN)
 
@@ -46,6 +48,7 @@ def tile_occurrencepool_pa_t_kernel(
 
         raw, grouped, h_codes, h_scales = {}, {}, {}, {}
         feat_acc, feat_grouped, feat_codes, feat_scales = {}, {}, {}, {}
+        feat_rows, feat_turned = {}, {}
         occ_hidden, occ_acc, occ_grouped, occ_codes, occ_scales = {}, {}, {}, {}, {}
         out_acc = {}
 
@@ -124,32 +127,32 @@ def tile_occurrencepool_pa_t_kernel(
                     stop=True,
                 )
 
-        def regroup(n):
-            grouped[n] = grouped_pool.tile(
-                [P, K_GROUPS, K_PASS, PACK], BF16, name="grouped", align_bytes=64
-            )
-            for g in range(K_GROUPS):
-                dst = grouped[n][:, g, :, :].rearrange("p (c i) j -> p c j i", i=4)
-                src = raw[(n, g)][:].rearrange("p j (c i) -> p c j i", i=4)
-                if n == 0:
-                    first = SCALAR_VOXELS_0
-                elif g < K_GROUPS - 1:
-                    first = K_PASS
-                else:
-                    first = K_PASS - GPSIMD_VOXELS
-                split = first // 4
-                nc.scalar.copy(out=dst[:, :split], in_=src[:, :split])
-                if n == 0:
-                    nc.vector.tensor_copy(out=dst[:, split:], in_=src[:, split:])
-                elif first < K_PASS:
-                    nc.gpsimd.tensor_scalar(
-                        out=grouped[n][:, g, first:, :],
-                        in0=raw[(n, g)][:, :, first:].rearrange("p j v -> p v j"),
-                        scalar1=1.0,
-                        scalar2=0.0,
-                        op0=mybir.AluOpType.mult,
-                        op1=mybir.AluOpType.add,
-                    )
+        def regroup(n, g):
+            if g == 0:
+                grouped[n] = grouped_pool.tile(
+                    [P, K_GROUPS, K_PASS, PACK], BF16, name="grouped", align_bytes=64
+                )
+            dst = grouped[n][:, g, :, :].rearrange("p (c i) j -> p c j i", i=4)
+            src = raw[(n, g)][:].rearrange("p j (c i) -> p c j i", i=4)
+            if n == 0:
+                first = SCALAR_VOXELS_0
+            elif g < K_GROUPS - 1:
+                first = K_PASS
+            else:
+                first = K_PASS - GPSIMD_VOXELS
+            split = first // 4
+            nc.scalar.copy(out=dst[:, :split], in_=src[:, :split])
+            if n == 0:
+                nc.vector.tensor_copy(out=dst[:, split:], in_=src[:, split:])
+            elif first < K_PASS:
+                nc.gpsimd.tensor_scalar(
+                    out=grouped[n][:, g, first:, :],
+                    in0=raw[(n, g)][:, :, first:].rearrange("p j v -> p v j"),
+                    scalar1=1.0,
+                    scalar2=0.0,
+                    op0=mybir.AluOpType.mult,
+                    op1=mybir.AluOpType.add,
+                )
 
         def quantise_h(n):
             h_codes[n] = work.tile([P, K_GROUPS, K_PASS], U32, name="h_codes", align_bytes=64)
@@ -177,16 +180,60 @@ def tile_occurrencepool_pa_t_kernel(
             feat_acc[(n, cb)] = acc
 
         def add_bias(n, cb):
-            if cb == 0:
-                feat_grouped[n] = work.tile(
-                    [P, C_IN, PACK], BF16, name="feat_grouped", align_bytes=64
-                )
             channels = slice(cb * P, (cb + 1) * P)
             nc.vector.tensor_tensor(
                 out=feat_grouped[n][:, channels, :],
                 in0=feat_acc[(n, cb)][:].rearrange("p t c -> p c t"),
                 in1=bias[:, channels].unsqueeze(2).to_broadcast([P, P, PACK]),
                 op=mybir.AluOpType.add,
+            )
+
+        bias_cols = consts.tile([P, SCALAR_BLOCKS], F32, name="bias_cols")
+
+        def bias_to_columns():
+            bias_t = occ_psum.tile([P, SCALAR_BLOCKS, P], BF16, name="bias_t", tag="occ_acc")
+            for i in range(SCALAR_BLOCKS):
+                cb = C_BLOCKS - SCALAR_BLOCKS + i
+                nc.tensor.transpose(
+                    bias_t[:, i, :], bias_row[:, cb * P : (cb + 1) * P], identity[:]
+                )
+            nc.scalar.copy(out=bias_cols[:], in_=bias_t[:, :, 0])
+
+        def rows_product(n, cb):
+            acc = feat_psum.tile([P, PACK, P], F32, name="feat_acc")
+            for g in range(K_GROUPS):
+                nc.tensor.matmul_mx(
+                    out=acc[:].rearrange("c t v -> c (t v)"),
+                    lhsT=w_words[:, g, 2 * P * cb : 2 * P * (cb + 1)].bitcast(FP4X4),
+                    lhsT_scale=w_scales[:, g, P * cb : P * (cb + 1)],
+                    rhs=h_codes[n][:, g, :].bitcast(FP8X4),
+                    rhs_scale=h_scales[n][:, g, :],
+                    start=(g == 0),
+                    stop=(g == K_GROUPS - 1),
+                )
+            feat_acc[(n, cb)] = acc
+
+        def add_bias_rows(n, cb):
+            feat_rows[(n, cb)] = work.tile([P, PACK, P], BF16, name="feat_rows")
+            column = cb - (C_BLOCKS - SCALAR_BLOCKS)
+            nc.scalar.activation(
+                out=feat_rows[(n, cb)][:],
+                in_=feat_acc[(n, cb)][:],
+                func=mybir.ActivationFunctionType.Identity,
+                bias=bias_cols[:, column : column + 1],
+                scale=1.0,
+            )
+
+        def turn_rows(n, cb):
+            turned = occ_psum.tile([P, PACK, P], BF16, name="turned", tag="occ_acc")
+            for t in range(PACK):
+                nc.tensor.transpose(turned[:, t, :], feat_rows[(n, cb)][:, t, :], identity[:])
+            feat_turned[(n, cb)] = turned
+
+        def regroup_rows(n, cb):
+            nc.scalar.copy(
+                out=feat_grouped[n][:, cb * P : (cb + 1) * P, :],
+                in_=feat_turned[(n, cb)][:].rearrange("p t c -> p c t"),
             )
 
         def quantise_feat(n):
@@ -249,28 +296,53 @@ def tile_occurrencepool_pa_t_kernel(
         def exists(n):
             return 0 <= n < ROUNDS
 
+        def vector_blocks(n):
+            return C_BLOCKS - (SCALAR_BLOCKS if n >= ROUNDS - TAIL_ROUNDS else 0)
+
+        def scalar_blocks(n):
+            return list(range(vector_blocks(n), C_BLOCKS)) if exists(n) else []
+
         for n in range(-2, ROUNDS):
             lead = 2 if n == 0 else 0
             for cb in range(lead):
                 add_bias(n, cb)
             if exists(n + 1):
+                feat_grouped[n + 1] = work.tile(
+                    [P, C_IN, PACK], BF16, name="feat_grouped", align_bytes=64
+                )
                 quantise_h(n + 1)
+                for cb in scalar_blocks(n + 1):
+                    rows_product(n + 1, cb)
                 for cb in range(lead + 1):
                     first_product(n + 1, cb)
-                occ_product(n + 1)
+                if n < 1:
+                    occ_product(n + 1)
             if exists(n + 2):
-                regroup(n + 2)
+                regroup(n + 2, 0)
+            for cb in scalar_blocks(n):
+                regroup_rows(n, cb)
+            if exists(n + 2):
+                regroup(n + 2, 1)
             if exists(n + 1):
                 occ_abs(n + 1)
+                for cb in scalar_blocks(n + 1):
+                    add_bias_rows(n + 1, cb)
+            to_turn = scalar_blocks(n + 1)
             for cb in range(lead, C_BLOCKS):
-                if exists(n):
+                if exists(n) and cb < vector_blocks(n):
                     add_bias(n, cb)
-                if exists(n + 1) and cb + 1 < C_BLOCKS:
+                if cb - lead < len(to_turn):
+                    turn_rows(n + 1, to_turn[cb - lead])
+                if exists(n + 1) and cb + 1 < vector_blocks(n + 1):
                     first_product(n + 1, cb + 1)
             if exists(n):
                 quantise_occ(n)
                 quantise_feat(n)
                 second_product(n)
+            if n >= 0 and exists(n + 2):
+                occ_product(n + 2)
+            if n == ROUNDS - TAIL_ROUNDS - 3:
+                bias_to_columns()
             if exists(n) and (n + 1) % ROUNDS_PER_SAMPLE == 0:
                 store_sample(n // ROUNDS_PER_SAMPLE)
             if exists(n + 2 + ROUNDS_IN_FLIGHT):

@@ -25,8 +25,10 @@ ROUNDS_IN_FLIGHT = 4
 GPSIMD_VOXELS = 320
 SCALAR_VOXELS_0 = 192
 WARM_UP = (4, 2)
-TAIL_ROUNDS = 2
-SCALAR_BLOCKS = 2
+LAST_PARTS = 2
+TAIL_BLOCKS = (2, 1)
+TAIL_ROUNDS = len(TAIL_BLOCKS)
+SCALAR_BLOCKS = max(TAIL_BLOCKS)
 
 FLOPS = 2 * SAMPLES * VOXELS * (C_IN * C_MID + MAPS * C_OCC + MAPS * C_IN)
 
@@ -42,9 +44,9 @@ def tile_occurrencepool_pa_t_kernel(
         raw_pool = ctx.enter_context(tc.tile_pool(name="raw", bufs=K_GROUPS * ROUNDS_IN_FLIGHT))
         work = ctx.enter_context(tc.tile_pool(name="work", bufs=3))
         grouped_pool = ctx.enter_context(tc.tile_pool(name="grouped_pool", bufs=2))
-        feat_psum = ctx.enter_context(tc.psum_pool(name="feat_psum", bufs=C_BLOCKS + 1))
+        feat_psum = ctx.enter_context(tc.psum_pool(name="feat_psum", bufs=C_BLOCKS))
         occ_psum = ctx.enter_context(tc.psum_pool(name="occ_psum", bufs=2))
-        out_psum = ctx.enter_context(tc.psum_pool(name="out_psum", bufs=1))
+        out_psum = ctx.enter_context(tc.psum_pool(name="out_psum", bufs=2))
 
         raw, grouped, h_codes, h_scales = {}, {}, {}, {}
         feat_acc, feat_grouped, feat_codes, feat_scales = {}, {}, {}, {}
@@ -239,11 +241,15 @@ def tile_occurrencepool_pa_t_kernel(
         def quantise_feat(n):
             feat_codes[n] = work.tile([P, C_IN], U32, name="feat_codes", align_bytes=64)
             feat_scales[n] = work.tile([P, C_IN], U8, name="feat_scales", align_bytes=64)
-            nc.vector.quantize_mx(
-                out=feat_codes[n][:].bitcast(FP8X4),
-                scales=feat_scales[n][:],
-                in_=feat_grouped[n][:].rearrange("p c t -> p (c t)"),
-            )
+            calls = LAST_PARTS if n == ROUNDS - 1 else 1
+            width = C_IN // calls
+            for i in range(calls):
+                channels = slice(i * width, (i + 1) * width)
+                nc.vector.quantize_mx(
+                    out=feat_codes[n][:, channels].bitcast(FP8X4),
+                    scales=feat_scales[n][:, channels],
+                    in_=feat_grouped[n][:, channels, :].rearrange("p c t -> p (c t)"),
+                )
 
         def occ_product(n):
             acc = occ_psum.tile([P, PACK, MAPS], F32, name="occ_acc")
@@ -274,30 +280,39 @@ def tile_occurrencepool_pa_t_kernel(
                 in_=occ_grouped[n][:].rearrange("p o t -> p (o t)"),
             )
 
+        def parts(b):
+            return LAST_PARTS if b == SAMPLES - 1 else 1
+
         def second_product(n):
             b, r = divmod(n, ROUNDS_PER_SAMPLE)
-            if r == 0:
-                out_acc[b] = out_psum.tile([MAPS, C_IN], F32, name="out_acc")
-            nc.tensor.matmul_mx(
-                out=out_acc[b][:],
-                lhsT=occ_codes[n][:].bitcast(FP8X4),
-                lhsT_scale=occ_scales[n][:],
-                rhs=feat_codes[n][:].bitcast(FP8X4),
-                rhs_scale=feat_scales[n][:],
-                start=(r == 0),
-                stop=(r == ROUNDS_PER_SAMPLE - 1),
-            )
+            width = C_IN // parts(b)
+            for i in range(parts(b)):
+                if r == 0:
+                    out_acc[(b, i)] = out_psum.tile([MAPS, width], F32, name="out_acc")
+                channels = slice(i * width, (i + 1) * width)
+                nc.tensor.matmul_mx(
+                    out=out_acc[(b, i)][:],
+                    lhsT=occ_codes[n][:].bitcast(FP8X4),
+                    lhsT_scale=occ_scales[n][:],
+                    rhs=feat_codes[n][:, channels].bitcast(FP8X4),
+                    rhs_scale=feat_scales[n][:, channels],
+                    start=(r == 0),
+                    stop=(r == ROUNDS_PER_SAMPLE - 1),
+                )
 
         def store_sample(b):
-            mean = work.tile([MAPS, C_IN], F32, name="mean")
-            nc.scalar.mul(out=mean[:], in_=out_acc[b][:], mul=1.0 / VOXELS)
-            nc.sync.dma_start(out=out[b], in_=mean[:])
+            width = C_IN // parts(b)
+            for i in range(parts(b)):
+                mean = work.tile([MAPS, width], F32, name="mean")
+                nc.scalar.mul(out=mean[:], in_=out_acc[(b, i)][:], mul=1.0 / VOXELS)
+                nc.sync.dma_start(out=out[b, :, i * width : (i + 1) * width], in_=mean[:])
 
         def exists(n):
             return 0 <= n < ROUNDS
 
         def vector_blocks(n):
-            return C_BLOCKS - (SCALAR_BLOCKS if n >= ROUNDS - TAIL_ROUNDS else 0)
+            first_tail_round = ROUNDS - TAIL_ROUNDS
+            return C_BLOCKS - (TAIL_BLOCKS[n - first_tail_round] if n >= first_tail_round else 0)
 
         def scalar_blocks(n):
             return list(range(vector_blocks(n), C_BLOCKS)) if exists(n) else []
@@ -327,14 +342,13 @@ def tile_occurrencepool_pa_t_kernel(
                 occ_abs(n + 1)
                 for cb in scalar_blocks(n + 1):
                     add_bias_rows(n + 1, cb)
-            to_turn = scalar_blocks(n + 1)
             for cb in range(lead, C_BLOCKS):
                 if exists(n) and cb < vector_blocks(n):
                     add_bias(n, cb)
-                if cb - lead < len(to_turn):
-                    turn_rows(n + 1, to_turn[cb - lead])
                 if exists(n + 1) and cb + 1 < vector_blocks(n + 1):
                     first_product(n + 1, cb + 1)
+            for cb in scalar_blocks(n + 1):
+                turn_rows(n + 1, cb)
             if exists(n):
                 quantise_occ(n)
                 quantise_feat(n)

@@ -22,9 +22,11 @@ ROUNDS = SAMPLES * ROUNDS_PER_SAMPLE
 C_BLOCKS = C_IN // P
 
 ROUNDS_IN_FLIGHT = 4
-GPSIMD_VOXELS = 320
+GPSIMD_VOXELS = 96
 SCALAR_VOXELS_0 = 192
 WARM_UP = (4, 2)
+SCALAR_EVERY = 3
+SCALAR_FIRST = 2
 LAST_PARTS = 2
 TAIL_BLOCKS = (2, 1)
 TAIL_ROUNDS = len(TAIL_BLOCKS)
@@ -117,6 +119,8 @@ def tile_occurrencepool_pa_t_kernel(
         nc.tensor.transpose(w_occ_acc[:], w_occ_rows[:], identity[:])
         w_occ_t = consts.tile([C_OCC, MAPS], BF16, name="w_occ_t")
         nc.vector.tensor_copy(out=w_occ_t[:], in_=w_occ_acc[:])
+        identity_words = consts.tile([P, P], F32, name="identity_words")
+        make_identity(nc, identity_words[:])
 
         warm_acc = feat_psum.tile([P, PACK, P], F32, name="feat_acc")
         for g in range(K_GROUPS):
@@ -141,7 +145,8 @@ def tile_occurrencepool_pa_t_kernel(
             elif g < K_GROUPS - 1:
                 first = K_PASS
             else:
-                first = K_PASS - GPSIMD_VOXELS
+                beside = vector_blocks(n - 3) if n >= 3 else C_BLOCKS - 1
+                first = K_PASS - GPSIMD_VOXELS * beside
             split = first // 4
             nc.scalar.copy(out=dst[:, :split], in_=src[:, :split])
             if n == 0:
@@ -192,14 +197,19 @@ def tile_occurrencepool_pa_t_kernel(
 
         bias_cols = consts.tile([P, SCALAR_BLOCKS], F32, name="bias_cols")
 
-        def bias_to_columns():
+        bias_turned = {}
+
+        def turn_bias():
             bias_t = occ_psum.tile([P, SCALAR_BLOCKS, P], BF16, name="bias_t", tag="occ_acc")
             for i in range(SCALAR_BLOCKS):
                 cb = C_BLOCKS - SCALAR_BLOCKS + i
                 nc.tensor.transpose(
                     bias_t[:, i, :], bias_row[:, cb * P : (cb + 1) * P], identity[:]
                 )
-            nc.scalar.copy(out=bias_cols[:], in_=bias_t[:, :, 0])
+            bias_turned[0] = bias_t
+
+        def copy_bias_columns():
+            nc.scalar.copy(out=bias_cols[:], in_=bias_turned[0][:, :, 0])
 
         def rows_product(n, cb):
             acc = feat_psum.tile([P, PACK, P], F32, name="feat_acc")
@@ -216,26 +226,30 @@ def tile_occurrencepool_pa_t_kernel(
             feat_acc[(n, cb)] = acc
 
         def add_bias_rows(n, cb):
-            feat_rows[(n, cb)] = work.tile([P, PACK, P], BF16, name="feat_rows")
+            feat_rows[(n, cb)] = work.tile([P, P, PACK], BF16, name="feat_rows")
             column = cb - (C_BLOCKS - SCALAR_BLOCKS)
             nc.scalar.activation(
                 out=feat_rows[(n, cb)][:],
-                in_=feat_acc[(n, cb)][:],
+                in_=feat_acc[(n, cb)][:].rearrange("c t p -> c p t"),
                 func=mybir.ActivationFunctionType.Identity,
                 bias=bias_cols[:, column : column + 1],
                 scale=1.0,
             )
 
         def turn_rows(n, cb):
-            turned = occ_psum.tile([P, PACK, P], BF16, name="turned", tag="occ_acc")
-            for t in range(PACK):
-                nc.tensor.transpose(turned[:, t, :], feat_rows[(n, cb)][:, t, :], identity[:])
+            words = feat_rows[(n, cb)][:].rearrange("c p t -> c (p t)").bitcast(F32)
+            turned = occ_psum.tile([P, PACK // 2, P], F32, name="turned", tag="occ_acc")
+            for u in range(PACK // 2):
+                nc.tensor.transpose(
+                    turned[:, u, :], words[:, u : P * PACK // 2 : PACK // 2], identity_words[:]
+                )
             feat_turned[(n, cb)] = turned
 
         def regroup_rows(n, cb):
+            block = feat_grouped[n][:, cb * P : (cb + 1) * P, :].rearrange("p c t -> p (c t)")
             nc.scalar.copy(
-                out=feat_grouped[n][:, cb * P : (cb + 1) * P, :],
-                in_=feat_turned[(n, cb)][:].rearrange("p t c -> p c t"),
+                out=block.bitcast(F32).rearrange("p (c u) -> p c u", u=PACK // 2),
+                in_=feat_turned[(n, cb)][:].rearrange("p u c -> p c u"),
             )
 
         def quantise_feat(n):
@@ -312,11 +326,16 @@ def tile_occurrencepool_pa_t_kernel(
 
         def vector_blocks(n):
             first_tail_round = ROUNDS - TAIL_ROUNDS
-            return C_BLOCKS - (TAIL_BLOCKS[n - first_tail_round] if n >= first_tail_round else 0)
+            if n >= first_tail_round:
+                return C_BLOCKS - TAIL_BLOCKS[n - first_tail_round]
+            if n >= SCALAR_FIRST and (n - SCALAR_FIRST) % SCALAR_EVERY == 0:
+                return C_BLOCKS - 1
+            return C_BLOCKS
 
         def scalar_blocks(n):
             return list(range(vector_blocks(n), C_BLOCKS)) if exists(n) else []
 
+        regroup(0, 0)
         for n in range(-2, ROUNDS):
             lead = 2 if n == 0 else 0
             for cb in range(lead):
@@ -333,15 +352,17 @@ def tile_occurrencepool_pa_t_kernel(
                 if n < 1:
                     occ_product(n + 1)
             if exists(n + 2):
-                regroup(n + 2, 0)
+                regroup(n + 2, 1)
             for cb in scalar_blocks(n):
                 regroup_rows(n, cb)
-            if exists(n + 2):
-                regroup(n + 2, 1)
+            if n == SCALAR_FIRST - 2:
+                copy_bias_columns()
             if exists(n + 1):
                 occ_abs(n + 1)
-                for cb in scalar_blocks(n + 1):
-                    add_bias_rows(n + 1, cb)
+            if exists(n + 3):
+                regroup(n + 3, 0)
+            for cb in scalar_blocks(n + 1):
+                add_bias_rows(n + 1, cb)
             for cb in range(lead, C_BLOCKS):
                 if exists(n) and cb < vector_blocks(n):
                     add_bias(n, cb)
@@ -355,8 +376,8 @@ def tile_occurrencepool_pa_t_kernel(
                 second_product(n)
             if n >= 0 and exists(n + 2):
                 occ_product(n + 2)
-            if n == ROUNDS - TAIL_ROUNDS - 3:
-                bias_to_columns()
+            if n == SCALAR_FIRST - 3:
+                turn_bias()
             if exists(n) and (n + 1) % ROUNDS_PER_SAMPLE == 0:
                 store_sample(n // ROUNDS_PER_SAMPLE)
             if exists(n + 2 + ROUNDS_IN_FLIGHT):

@@ -28,7 +28,7 @@ WARM_UP = (4, 2)
 SCALAR_EVERY = 3
 SCALAR_FIRST = 2
 LAST_PARTS = 2
-TAIL_BLOCKS = (2, 1)
+TAIL_BLOCKS = (2, 2)
 TAIL_ROUNDS = len(TAIL_BLOCKS)
 SCALAR_BLOCKS = max(TAIL_BLOCKS)
 

@@ -29,6 +29,7 @@ SCALAR_EVERY = 3
 SCALAR_FIRST = 2
 LAST_PARTS = 2
 TAIL_BLOCKS = (2, 2)
+FEAT_CALLS = 2
 TAIL_ROUNDS = len(TAIL_BLOCKS)
 SCALAR_BLOCKS = max(TAIL_BLOCKS)
 
@@ -255,9 +256,10 @@ def tile_occurrencepool_pa_t_kernel(
         def quantise_feat(n):
             feat_codes[n] = work.tile([P, C_IN], U32, name="feat_codes", align_bytes=64)
             feat_scales[n] = work.tile([P, C_IN], U8, name="feat_scales", align_bytes=64)
-            calls = LAST_PARTS if n == ROUNDS - 1 else 1
-            width = C_IN // calls
-            for i in range(calls):
+            width = C_IN // FEAT_CALLS
+            for i in range(FEAT_CALLS):
+                if i == 1:
+                    quantise_occ(n)
                 channels = slice(i * width, (i + 1) * width)
                 nc.vector.quantize_mx(
                     out=feat_codes[n][:, channels].bitcast(FP8X4),
@@ -371,7 +373,6 @@ def tile_occurrencepool_pa_t_kernel(
             for cb in scalar_blocks(n + 1):
                 turn_rows(n + 1, cb)
             if exists(n):
-                quantise_occ(n)
                 quantise_feat(n)
                 second_product(n)
             if n >= 0 and exists(n + 2):

@@ -22,7 +22,7 @@ ROUNDS = SAMPLES * ROUNDS_PER_SAMPLE
 C_BLOCKS = C_IN // P
 
 ROUNDS_IN_FLIGHT = 4
-GPSIMD_VOXELS = 96
+GPSIMD_VOXELS = 112
 SCALAR_VOXELS_0 = 192
 WARM_UP = (4, 2)
 SCALAR_EVERY = 3
@@ -154,8 +154,8 @@ def tile_occurrencepool_pa_t_kernel(
                 nc.vector.tensor_copy(out=dst[:, split:], in_=src[:, split:])
             elif first < K_PASS:
                 nc.gpsimd.tensor_scalar(
-                    out=grouped[n][:, g, first:, :],
-                    in0=raw[(n, g)][:, :, first:].rearrange("p j v -> p v j"),
+                    out=dst[:, split:],
+                    in0=src[:, split:],
                     scalar1=1.0,
                     scalar2=0.0,
                     op0=mybir.AluOpType.mult,

@@ -22,7 +22,7 @@ ROUNDS = SAMPLES * ROUNDS_PER_SAMPLE
 C_BLOCKS = C_IN // P
 
 ROUNDS_IN_FLIGHT = 4
-GPSIMD_VOXELS = 112
+GPSIMD_VOXELS = 96
 SCALAR_VOXELS_0 = 192
 WARM_UP = (4, 2)
 SCALAR_EVERY = 3

@@ -141,6 +141,8 @@ def tile_occurrencepool_pa_t_kernel(
                 )
             dst = grouped[n][:, g, :, :].rearrange("p (c i) j -> p c j i", i=4)
             src = raw[(n, g)][:].rearrange("p j (c i) -> p c j i", i=4)
+            pair_dst = grouped[n][:, g, :, :].rearrange("p (c i) j -> p c j i", i=2)
+            pair_src = raw[(n, g)][:].rearrange("p j (c i) -> p c j i", i=2)
             if n == 0:
                 first = SCALAR_VOXELS_0
             elif g < K_GROUPS - 1:
@@ -149,7 +151,7 @@ def tile_occurrencepool_pa_t_kernel(
                 beside = vector_blocks(n - 3) if n >= 3 else C_BLOCKS - 1
                 first = K_PASS - GPSIMD_VOXELS * beside
             split = first // 4
-            nc.scalar.copy(out=dst[:, :split], in_=src[:, :split])
+            nc.scalar.copy(out=pair_dst[:, : first // 2], in_=pair_src[:, : first // 2])
             if n == 0:
                 nc.vector.tensor_copy(out=dst[:, split:], in_=src[:, split:])
             elif first < K_PASS:

@@ -22,13 +22,13 @@ ROUNDS = SAMPLES * ROUNDS_PER_SAMPLE
 C_BLOCKS = C_IN // P
 
 ROUNDS_IN_FLIGHT = 4
-GPSIMD_VOXELS = 96
+GPSIMD_VOXELS = 104
 SCALAR_VOXELS_0 = 192
 WARM_UP = (4, 2)
 SCALAR_EVERY = 3
 SCALAR_FIRST = 2
 LAST_PARTS = 2
-TAIL_BLOCKS = (2, 2)
+TAIL_BLOCKS = (1, 2, 2)
 FEAT_CALLS = 2
 TAIL_ROUNDS = len(TAIL_BLOCKS)
 SCALAR_BLOCKS = max(TAIL_BLOCKS)
@@ -112,14 +112,12 @@ def tile_occurrencepool_pa_t_kernel(
         bias_acc = occ_psum.tile([P, C_IN], F32, name="bias_acc", tag="occ_acc")
         nc.tensor.matmul(out=bias_acc[:], lhsT=ones[:], rhs=bias_row[:], start=True, stop=True)
         bias = consts.tile([P, C_IN], F32, name="bias")
-        nc.vector.tensor_copy(out=bias[:], in_=bias_acc[:])
 
         identity = consts.tile([P, P], BF16, name="identity")
         make_identity(nc, identity[:])
         w_occ_acc = occ_psum.tile([C_OCC, MAPS], BF16, name="w_occ_acc", tag="occ_acc")
         nc.tensor.transpose(w_occ_acc[:], w_occ_rows[:], identity[:])
         w_occ_t = consts.tile([C_OCC, MAPS], BF16, name="w_occ_t")
-        nc.vector.tensor_copy(out=w_occ_t[:], in_=w_occ_acc[:])
         identity_words = consts.tile([P, P], F32, name="identity_words")
         make_identity(nc, identity_words[:])
 
@@ -149,12 +147,12 @@ def tile_occurrencepool_pa_t_kernel(
                 first = K_PASS
             else:
                 beside = vector_blocks(n - 3) if n >= 3 else C_BLOCKS - 1
-                first = K_PASS - GPSIMD_VOXELS * beside
+                first = K_PASS - (256 if n == 4 else 256 if n == 2 else GPSIMD_VOXELS * beside)
             split = first // 4
             nc.scalar.copy(out=pair_dst[:, : first // 2], in_=pair_src[:, : first // 2])
             if n == 0:
                 nc.vector.tensor_copy(out=dst[:, split:], in_=src[:, split:])
-            elif first < K_PASS:
+            elif first < K_PASS and n != 4:
                 nc.gpsimd.tensor_scalar(
                     out=dst[:, split:],
                     in0=src[:, split:],
@@ -163,6 +161,13 @@ def tile_occurrencepool_pa_t_kernel(
                     op0=mybir.AluOpType.mult,
                     op1=mybir.AluOpType.add,
                 )
+
+        def vector_regroup():
+            first = K_PASS - 256
+            nc.vector.tensor_copy(
+                out=grouped[4][:, 1, first:, :].rearrange("p (c i) j -> p c j i", i=4),
+                in_=raw[(4, 1)][:, :, first:].rearrange("p j (c i) -> p c j i", i=4),
+            )
 
         def quantise_h(n):
             h_codes[n] = work.tile([P, K_GROUPS, K_PASS], U32, name="h_codes", align_bytes=64)
@@ -259,8 +264,9 @@ def tile_occurrencepool_pa_t_kernel(
             feat_codes[n] = work.tile([P, C_IN], U32, name="feat_codes", align_bytes=64)
             feat_scales[n] = work.tile([P, C_IN], U8, name="feat_scales", align_bytes=64)
             width = C_IN // FEAT_CALLS
+            between = 1 if vector_blocks(n) > C_BLOCKS // FEAT_CALLS else 0
             for i in range(FEAT_CALLS):
-                if i == 1:
+                if i == between:
                     quantise_occ(n)
                 channels = slice(i * width, (i + 1) * width)
                 nc.vector.quantize_mx(
@@ -348,12 +354,17 @@ def tile_occurrencepool_pa_t_kernel(
                 feat_grouped[n + 1] = work.tile(
                     [P, C_IN, PACK], BF16, name="feat_grouped", align_bytes=64
                 )
+                if n == 2:
+                    vector_regroup()
                 quantise_h(n + 1)
+                if n == -1:
+                    nc.vector.tensor_copy(out=bias[:], in_=bias_acc[:])
+                    nc.vector.tensor_copy(out=w_occ_t[:], in_=w_occ_acc[:])
                 for cb in scalar_blocks(n + 1):
                     rows_product(n + 1, cb)
                 for cb in range(lead + 1):
                     first_product(n + 1, cb)
-                if n < 1:
+                if n < 0:
                     occ_product(n + 1)
             if exists(n + 2):
                 regroup(n + 2, 1)
@@ -367,6 +378,8 @@ def tile_occurrencepool_pa_t_kernel(
                 regroup(n + 3, 0)
             for cb in scalar_blocks(n + 1):
                 add_bias_rows(n + 1, cb)
+            if n > 0 and n % ROUNDS_PER_SAMPLE == 0:
+                store_sample(n // ROUNDS_PER_SAMPLE - 1)
             for cb in range(lead, C_BLOCKS):
                 if exists(n) and cb < vector_blocks(n):
                     add_bias(n, cb)
@@ -377,11 +390,11 @@ def tile_occurrencepool_pa_t_kernel(
             if exists(n):
                 quantise_feat(n)
                 second_product(n)
-            if n >= 0 and exists(n + 2):
+            if n >= -1 and exists(n + 2):
                 occ_product(n + 2)
             if n == SCALAR_FIRST - 3:
                 turn_bias()
-            if exists(n) and (n + 1) % ROUNDS_PER_SAMPLE == 0:
-                store_sample(n // ROUNDS_PER_SAMPLE)
+            if n == ROUNDS - 1:
+                store_sample(SAMPLES - 1)
             if exists(n + 2 + ROUNDS_IN_FLIGHT):
                 load_round(n + 2 + ROUNDS_IN_FLIGHT)

@@ -27,9 +27,8 @@ SCALAR_VOXELS_0 = 192
 WARM_UP = (4, 2)
 SCALAR_EVERY = 3
 SCALAR_FIRST = 2
-LAST_PARTS = 2
+LAST_PARTS = ((0, 256), (256, 384), (384, 512))
 TAIL_BLOCKS = (1, 2, 2)
-FEAT_CALLS = 2
 TAIL_ROUNDS = len(TAIL_BLOCKS)
 SCALAR_BLOCKS = max(TAIL_BLOCKS)
 
@@ -46,6 +45,7 @@ def tile_occurrencepool_pa_t_kernel(
         occ_in = ctx.enter_context(tc.tile_pool(name="occ_in", bufs=ROUNDS_IN_FLIGHT))
         raw_pool = ctx.enter_context(tc.tile_pool(name="raw", bufs=K_GROUPS * ROUNDS_IN_FLIGHT))
         work = ctx.enter_context(tc.tile_pool(name="work", bufs=3))
+        codes_pool = ctx.enter_context(tc.tile_pool(name="codes_pool", bufs=4))
         grouped_pool = ctx.enter_context(tc.tile_pool(name="grouped_pool", bufs=2))
         feat_psum = ctx.enter_context(tc.psum_pool(name="feat_psum", bufs=C_BLOCKS))
         occ_psum = ctx.enter_context(tc.psum_pool(name="occ_psum", bufs=2))
@@ -234,22 +234,22 @@ def tile_occurrencepool_pa_t_kernel(
             feat_acc[(n, cb)] = acc
 
         def add_bias_rows(n, cb):
-            feat_rows[(n, cb)] = work.tile([P, P, PACK], BF16, name="feat_rows")
+            feat_rows[(n, cb)] = work.tile([P, PACK // 2, P, 2], BF16, name="feat_rows")
             column = cb - (C_BLOCKS - SCALAR_BLOCKS)
             nc.scalar.activation(
                 out=feat_rows[(n, cb)][:],
-                in_=feat_acc[(n, cb)][:].rearrange("c t p -> c p t"),
+                in_=feat_acc[(n, cb)][:].rearrange("c (u e) p -> c u p e", e=2),
                 func=mybir.ActivationFunctionType.Identity,
                 bias=bias_cols[:, column : column + 1],
                 scale=1.0,
             )
 
         def turn_rows(n, cb):
-            words = feat_rows[(n, cb)][:].rearrange("c p t -> c (p t)").bitcast(F32)
+            words = feat_rows[(n, cb)][:].rearrange("c u p e -> c (u p e)").bitcast(F32)
             turned = occ_psum.tile([P, PACK // 2, P], F32, name="turned", tag="occ_acc")
             for u in range(PACK // 2):
                 nc.tensor.transpose(
-                    turned[:, u, :], words[:, u : P * PACK // 2 : PACK // 2], identity_words[:]
+                    turned[:, u, :], words[:, u * P : (u + 1) * P], identity_words[:]
                 )
             feat_turned[(n, cb)] = turned
 
@@ -261,14 +261,14 @@ def tile_occurrencepool_pa_t_kernel(
             )
 
         def quantise_feat(n):
-            feat_codes[n] = work.tile([P, C_IN], U32, name="feat_codes", align_bytes=64)
-            feat_scales[n] = work.tile([P, C_IN], U8, name="feat_scales", align_bytes=64)
-            width = C_IN // FEAT_CALLS
-            between = 1 if vector_blocks(n) > C_BLOCKS // FEAT_CALLS else 0
-            for i in range(FEAT_CALLS):
+            feat_codes[n] = codes_pool.tile([P, C_IN], U32, name="feat_codes", align_bytes=64)
+            feat_scales[n] = codes_pool.tile([P, C_IN], U8, name="feat_scales", align_bytes=64)
+            between = 1 if vector_blocks(n) > 2 else 0
+            calls = LAST_PARTS if n == ROUNDS - 1 else ((0, C_IN // 2), (C_IN // 2, C_IN))
+            for i, (lo, hi) in enumerate(calls):
                 if i == between:
                     quantise_occ(n)
-                channels = slice(i * width, (i + 1) * width)
+                channels = slice(lo, hi)
                 nc.vector.quantize_mx(
                     out=feat_codes[n][:, channels].bitcast(FP8X4),
                     scales=feat_scales[n][:, channels],
@@ -288,36 +288,64 @@ def tile_occurrencepool_pa_t_kernel(
             occ_acc[n] = acc
 
         def occ_abs(n):
-            occ_grouped[n] = work.tile([P, MAPS, PACK], BF16, name="occ_grouped", align_bytes=64)
+            if n % 2 == 0:
+                occ_grouped[n] = work.tile([P, 2, MAPS, PACK], BF16, name="occ_grouped", align_bytes=64)
+                occ_grouped[n + 1] = occ_grouped[n]
             nc.scalar.activation(
-                out=occ_grouped[n][:],
+                out=occ_grouped[n][:, n % 2, :, :],
                 in_=occ_acc[n][:].rearrange("p t o -> p o t"),
                 func=mybir.ActivationFunctionType.Abs,
             )
 
+        def occ_due(n):
+            if n >= ROUNDS - 2:
+                return [n]
+            return [n - 1, n] if n % 2 == 1 else []
+
         def quantise_occ(n):
-            occ_codes[n] = work.tile([P, MAPS], U32, name="occ_codes", align_bytes=64)
-            occ_scales[n] = work.tile([P, MAPS], U8, name="occ_scales", align_bytes=64)
+            rounds = occ_due(n)
+            if not rounds:
+                return
+            first = rounds[0] % 2
+            count = len(rounds)
+            codes = codes_pool.tile([P, count, MAPS], U32, name="occ_codes", align_bytes=64)
+            scales = codes_pool.tile([P, count, MAPS], U8, name="occ_scales", align_bytes=64)
             nc.vector.quantize_mx(
-                out=occ_codes[n][:].bitcast(FP8X4),
-                scales=occ_scales[n][:],
-                in_=occ_grouped[n][:].rearrange("p o t -> p (o t)"),
+                out=codes[:].rearrange("p r o -> p (r o)").bitcast(FP8X4),
+                scales=scales[:].rearrange("p r o -> p (r o)"),
+                in_=occ_grouped[n][:, first : first + count, :, :].rearrange("p r o t -> p (r o t)"),
             )
+            for i, m in enumerate(rounds):
+                occ_codes[m] = codes[:, i, :]
+                occ_scales[m] = scales[:, i, :]
 
         def parts(b):
-            return LAST_PARTS if b == SAMPLES - 1 else 1
+            return LAST_PARTS if b == SAMPLES - 1 else ((0, C_IN),)
 
         def second_product(n):
             b, r = divmod(n, ROUNDS_PER_SAMPLE)
-            width = C_IN // parts(b)
-            for i in range(parts(b)):
+            ranges = parts(b)
+            if n == ROUNDS - 1:
+                for m in range(n - r, n):
+                    sum_up(m, b, len(ranges) - 1)
+            for i in range(len(ranges)):
+                if b < SAMPLES - 1 or i < len(ranges) - 1 or n == ROUNDS - 1:
+                    sum_up(n, b, i)
+
+        def sum_up(n, b, i):
+                r = n % ROUNDS_PER_SAMPLE
+                lo, hi = parts(b)[i]
                 if r == 0:
-                    out_acc[(b, i)] = out_psum.tile([MAPS, width], F32, name="out_acc")
-                channels = slice(i * width, (i + 1) * width)
+                    late = b == SAMPLES - 1 and i == len(parts(b)) - 1
+                    pool = feat_psum if late else out_psum
+                    out_acc[(b, i)] = pool.tile(
+                        [MAPS, hi - lo], F32, name="out_acc", tag="feat_acc" if late else "out_acc"
+                    )
+                channels = slice(lo, hi)
                 nc.tensor.matmul_mx(
                     out=out_acc[(b, i)][:],
-                    lhsT=occ_codes[n][:].bitcast(FP8X4),
-                    lhsT_scale=occ_scales[n][:],
+                    lhsT=occ_codes[n].bitcast(FP8X4),
+                    lhsT_scale=occ_scales[n],
                     rhs=feat_codes[n][:, channels].bitcast(FP8X4),
                     rhs_scale=feat_scales[n][:, channels],
                     start=(r == 0),
@@ -325,11 +353,10 @@ def tile_occurrencepool_pa_t_kernel(
                 )
 
         def store_sample(b):
-            width = C_IN // parts(b)
-            for i in range(parts(b)):
-                mean = work.tile([MAPS, width], F32, name="mean")
+            for i, (lo, hi) in enumerate(parts(b)):
+                mean = work.tile([MAPS, hi - lo], F32, name="mean")
                 nc.scalar.mul(out=mean[:], in_=out_acc[(b, i)][:], mul=1.0 / VOXELS)
-                nc.sync.dma_start(out=out[b, :, i * width : (i + 1) * width], in_=mean[:])
+                nc.sync.dma_start(out=out[b, :, lo:hi], in_=mean[:])
 
         def exists(n):
             return 0 <= n < ROUNDS
@@ -389,7 +416,8 @@ def tile_occurrencepool_pa_t_kernel(
                 turn_rows(n + 1, cb)
             if exists(n):
                 quantise_feat(n)
-                second_product(n)
+                for m in occ_due(n):
+                    second_product(m)
             if n >= -1 and exists(n + 2):
                 occ_product(n + 2)
             if n == SCALAR_FIRST - 3:

@@ -22,7 +22,7 @@ ROUNDS = SAMPLES * ROUNDS_PER_SAMPLE
 C_BLOCKS = C_IN // P
 
 ROUNDS_IN_FLIGHT = 4
-GPSIMD_VOXELS = 104
+GPSIMD_VOXELS = 100
 SCALAR_VOXELS_0 = 192
 WARM_UP = (4, 2)
 SCALAR_EVERY = 3

from contextlib import ExitStack

import concourse.mybir as mybir
from concourse.masks import make_identity

BF16 = mybir.dt.bfloat16
F32 = mybir.dt.float32
I32 = mybir.dt.int32
U32 = mybir.dt.uint32
U8 = mybir.dt.uint8
FP8X4 = mybir.dt.float8_e4m3fn_x4
FP4X4 = mybir.dt.float4_e2m1fn_x4

P = 128
PACK = 4
K_PASS = P * PACK

SAMPLES, C_MID, C_IN, C_OCC, MAPS, VOXELS = 4, 1024, 512, 128, 128, 2048
K_GROUPS = C_MID // K_PASS
ROUNDS_PER_SAMPLE = VOXELS // K_PASS
ROUNDS = SAMPLES * ROUNDS_PER_SAMPLE
C_BLOCKS = C_IN // P

ROUNDS_IN_FLIGHT = 4
GPSIMD_VOXELS = 100
SCALAR_VOXELS_0 = 192
WARM_UP = (4, 2)
SCALAR_EVERY = 3
SCALAR_FIRST = 2
LAST_PARTS = ((0, 256), (256, 384), (384, 512))
TAIL_BLOCKS = (1, 2, 2)
TAIL_ROUNDS = len(TAIL_BLOCKS)
SCALAR_BLOCKS = max(TAIL_BLOCKS)

FLOPS = 2 * SAMPLES * VOXELS * (C_IN * C_MID + MAPS * C_OCC + MAPS * C_IN)


def tile_occurrencepool_pa_t_kernel(
    tc, h_add, w_add2_words, w_add2_scales, b_add2, h_occ, w_occ3, out
):
    nc = tc.nc
    with ExitStack() as ctx:
        ctx.enter_context(tc.manual_schedule())
        consts = ctx.enter_context(tc.tile_pool(name="consts", bufs=1))
        occ_in = ctx.enter_context(tc.tile_pool(name="occ_in", bufs=ROUNDS_IN_FLIGHT))
        raw_pool = ctx.enter_context(tc.tile_pool(name="raw", bufs=K_GROUPS * ROUNDS_IN_FLIGHT))
        work = ctx.enter_context(tc.tile_pool(name="work", bufs=3))
        codes_pool = ctx.enter_context(tc.tile_pool(name="codes_pool", bufs=4))
        grouped_pool = ctx.enter_context(tc.tile_pool(name="grouped_pool", bufs=2))
        feat_psum = ctx.enter_context(tc.psum_pool(name="feat_psum", bufs=C_BLOCKS))
        occ_psum = ctx.enter_context(tc.psum_pool(name="occ_psum", bufs=2))
        out_psum = ctx.enter_context(tc.psum_pool(name="out_psum", bufs=2))

        raw, grouped, h_codes, h_scales = {}, {}, {}, {}
        feat_acc, feat_grouped, feat_codes, feat_scales = {}, {}, {}, {}
        feat_rows, feat_turned = {}, {}
        occ_hidden, occ_acc, occ_grouped, occ_codes, occ_scales = {}, {}, {}, {}, {}
        out_acc = {}

        def load_h(n, g):
            b, r = divmod(n, ROUNDS_PER_SAMPLE)
            rows = h_add[b, g * K_PASS : (g + 1) * K_PASS, r * K_PASS : (r + 1) * K_PASS]
            raw[(n, g)] = raw_pool.tile([P, PACK, K_PASS], BF16, name="raw")
            nc.sync.dma_start(out=raw[(n, g)][:], in_=rows.rearrange("(p j) v -> p j v", j=PACK))

        def load_hidden(n):
            b, r = divmod(n, ROUNDS_PER_SAMPLE)
            occ_hidden[n] = occ_in.tile([C_OCC, K_PASS], BF16, name="hidden")
            nc.sync.dma_start(
                out=occ_hidden[n][:], in_=h_occ[b, :, r * K_PASS : (r + 1) * K_PASS]
            )

        def load_round(n):
            for g in range(K_GROUPS):
                load_h(n, g)
            load_hidden(n)

        w_occ_rows = consts.tile([MAPS, C_OCC], BF16, name="w_occ_rows")
        nc.sync.dma_start(out=w_occ_rows[:], in_=w_occ3)
        bias_row = consts.tile([P, C_IN], BF16, name="bias_row")
        nc.vector.memset(bias_row[:], 0.0)
        nc.sync.dma_start(out=bias_row[0:1, :], in_=b_add2.unsqueeze(0))
        ones = consts.tile([P, P], BF16, name="ones")
        nc.vector.memset(ones[:], 1.0)

        load_h(0, 0)
        load_h(0, 1)
        load_h(1, 0)

        w_words = consts.tile([P, K_GROUPS, 2 * C_IN], U8, name="w_words", align_bytes=64)
        nc.sync.dma_start(
            out=w_words[:].bitcast(I32),
            in_=w_add2_words.bitcast(I32).rearrange("g p n -> p g n"),
        )
        w_scales = consts.tile([P, K_GROUPS, C_IN], U8, name="w_scales", align_bytes=64)
        nc.vector.memset(w_scales[:].bitcast(I32), 0)
        scale_rows = w_add2_scales.bitcast(I32).rearrange("g (q s) n -> s q g n", s=4)
        for s in range(4):
            nc.sync.dma_start(out=w_scales[s:P:32, :, :].bitcast(I32), in_=scale_rows[s])

        load_hidden(0)
        load_h(1, 1)
        load_hidden(1)
        for n in range(2, ROUNDS_IN_FLIGHT):
            load_round(n)

        warm = consts.tile([P, 1], F32, name="warm")
        nc.scalar.activation(
            out=warm[:], in_=ones[:, 0:1], func=mybir.ActivationFunctionType.Abs
        )

        bias_acc = occ_psum.tile([P, C_IN], F32, name="bias_acc", tag="occ_acc")
        nc.tensor.matmul(out=bias_acc[:], lhsT=ones[:], rhs=bias_row[:], start=True, stop=True)
        bias = consts.tile([P, C_IN], F32, name="bias")

        identity = consts.tile([P, P], BF16, name="identity")
        make_identity(nc, identity[:])
        w_occ_acc = occ_psum.tile([C_OCC, MAPS], BF16, name="w_occ_acc", tag="occ_acc")
        nc.tensor.transpose(w_occ_acc[:], w_occ_rows[:], identity[:])
        w_occ_t = consts.tile([C_OCC, MAPS], BF16, name="w_occ_t")
        identity_words = consts.tile([P, P], F32, name="identity_words")
        make_identity(nc, identity_words[:])

        warm_acc = feat_psum.tile([P, PACK, P], F32, name="feat_acc")
        for g in range(K_GROUPS):
            for j in range(WARM_UP[g]):
                nc.tensor.matmul(
                    out=warm_acc[:].rearrange("p t c -> p (t c)"),
                    lhsT=ones[:],
                    rhs=raw[(0, g)][:, j, :],
                    start=True,
                    stop=True,
                )

        def regroup(n, g):
            if g == 0:
                grouped[n] = grouped_pool.tile(
                    [P, K_GROUPS, K_PASS, PACK], BF16, name="grouped", align_bytes=64
                )
            dst = grouped[n][:, g, :, :].rearrange("p (c i) j -> p c j i", i=4)
            src = raw[(n, g)][:].rearrange("p j (c i) -> p c j i", i=4)
            pair_dst = grouped[n][:, g, :, :].rearrange("p (c i) j -> p c j i", i=2)
            pair_src = raw[(n, g)][:].rearrange("p j (c i) -> p c j i", i=2)
            if n == 0:
                first = SCALAR_VOXELS_0
            elif g < K_GROUPS - 1:
                first = K_PASS
            else:
                beside = vector_blocks(n - 3) if n >= 3 else C_BLOCKS - 1
                first = K_PASS - (256 if n == 4 else 256 if n == 2 else GPSIMD_VOXELS * beside)
            split = first // 4
            nc.scalar.copy(out=pair_dst[:, : first // 2], in_=pair_src[:, : first // 2])
            if n == 0:
                nc.vector.tensor_copy(out=dst[:, split:], in_=src[:, split:])
            elif first < K_PASS and n != 4:
                nc.gpsimd.tensor_scalar(
                    out=dst[:, split:],
                    in0=src[:, split:],
                    scalar1=1.0,
                    scalar2=0.0,
                    op0=mybir.AluOpType.mult,
                    op1=mybir.AluOpType.add,
                )

        def vector_regroup():
            first = K_PASS - 256
            nc.vector.tensor_copy(
                out=grouped[4][:, 1, first:, :].rearrange("p (c i) j -> p c j i", i=4),
                in_=raw[(4, 1)][:, :, first:].rearrange("p j (c i) -> p c j i", i=4),
            )

        def quantise_h(n):
            h_codes[n] = work.tile([P, K_GROUPS, K_PASS], U32, name="h_codes", align_bytes=64)
            h_scales[n] = work.tile([P, K_GROUPS, K_PASS], U8, name="h_scales", align_bytes=64)
            nc.vector.quantize_mx(
                out=h_codes[n][:].rearrange("p g v -> p (g v)").bitcast(FP8X4),
                scales=h_scales[n][:].rearrange("p g v -> p (g v)"),
                in_=grouped[n][:].rearrange("p g v j -> p (g v j)"),
            )

        def first_product(n, cb):
            acc = feat_psum.tile([P, PACK, P], F32, name="feat_acc")
            for t in range(PACK):
                voxels = slice(t * P, (t + 1) * P)
                for g in range(K_GROUPS):
                    nc.tensor.matmul_mx(
                        out=acc[:, t, :],
                        lhsT=h_codes[n][:, g, voxels].bitcast(FP8X4),
                        lhsT_scale=h_scales[n][:, g, voxels],
                        rhs=w_words[:, g, 2 * P * cb : 2 * P * (cb + 1)].bitcast(FP4X4),
                        rhs_scale=w_scales[:, g, P * cb : P * (cb + 1)],
                        start=(g == 0),
                        stop=(g == K_GROUPS - 1),
                    )
            feat_acc[(n, cb)] = acc

        def add_bias(n, cb):
            channels = slice(cb * P, (cb + 1) * P)
            nc.vector.tensor_tensor(
                out=feat_grouped[n][:, channels, :],
                in0=feat_acc[(n, cb)][:].rearrange("p t c -> p c t"),
                in1=bias[:, channels].unsqueeze(2).to_broadcast([P, P, PACK]),
                op=mybir.AluOpType.add,
            )

        bias_cols = consts.tile([P, SCALAR_BLOCKS], F32, name="bias_cols")

        bias_turned = {}

        def turn_bias():
            bias_t = occ_psum.tile([P, SCALAR_BLOCKS, P], BF16, name="bias_t", tag="occ_acc")
            for i in range(SCALAR_BLOCKS):
                cb = C_BLOCKS - SCALAR_BLOCKS + i
                nc.tensor.transpose(
                    bias_t[:, i, :], bias_row[:, cb * P : (cb + 1) * P], identity[:]
                )
            bias_turned[0] = bias_t

        def copy_bias_columns():
            nc.scalar.copy(out=bias_cols[:], in_=bias_turned[0][:, :, 0])

        def rows_product(n, cb):
            acc = feat_psum.tile([P, PACK, P], F32, name="feat_acc")
            for g in range(K_GROUPS):
                nc.tensor.matmul_mx(
                    out=acc[:].rearrange("c t v -> c (t v)"),
                    lhsT=w_words[:, g, 2 * P * cb : 2 * P * (cb + 1)].bitcast(FP4X4),
                    lhsT_scale=w_scales[:, g, P * cb : P * (cb + 1)],
                    rhs=h_codes[n][:, g, :].bitcast(FP8X4),
                    rhs_scale=h_scales[n][:, g, :],
                    start=(g == 0),
                    stop=(g == K_GROUPS - 1),
                )
            feat_acc[(n, cb)] = acc

        def add_bias_rows(n, cb):
            feat_rows[(n, cb)] = work.tile([P, PACK // 2, P, 2], BF16, name="feat_rows")
            column = cb - (C_BLOCKS - SCALAR_BLOCKS)
            nc.scalar.activation(
                out=feat_rows[(n, cb)][:],
                in_=feat_acc[(n, cb)][:].rearrange("c (u e) p -> c u p e", e=2),
                func=mybir.ActivationFunctionType.Identity,
                bias=bias_cols[:, column : column + 1],
                scale=1.0,
            )

        def turn_rows(n, cb):
            words = feat_rows[(n, cb)][:].rearrange("c u p e -> c (u p e)").bitcast(F32)
            turned = occ_psum.tile([P, PACK // 2, P], F32, name="turned", tag="occ_acc")
            for u in range(PACK // 2):
                nc.tensor.transpose(
                    turned[:, u, :], words[:, u * P : (u + 1) * P], identity_words[:]
                )
            feat_turned[(n, cb)] = turned

        def regroup_rows(n, cb):
            block = feat_grouped[n][:, cb * P : (cb + 1) * P, :].rearrange("p c t -> p (c t)")
            nc.scalar.copy(
                out=block.bitcast(F32).rearrange("p (c u) -> p c u", u=PACK // 2),
                in_=feat_turned[(n, cb)][:].rearrange("p u c -> p c u"),
            )

        def quantise_feat(n):
            feat_codes[n] = codes_pool.tile([P, C_IN], U32, name="feat_codes", align_bytes=64)
            feat_scales[n] = codes_pool.tile([P, C_IN], U8, name="feat_scales", align_bytes=64)
            between = 1 if vector_blocks(n) > 2 else 0
            calls = LAST_PARTS if n == ROUNDS - 1 else ((0, C_IN // 2), (C_IN // 2, C_IN))
            for i, (lo, hi) in enumerate(calls):
                if i == between:
                    quantise_occ(n)
                channels = slice(lo, hi)
                nc.vector.quantize_mx(
                    out=feat_codes[n][:, channels].bitcast(FP8X4),
                    scales=feat_scales[n][:, channels],
                    in_=feat_grouped[n][:, channels, :].rearrange("p c t -> p (c t)"),
                )

        def occ_product(n):
            acc = occ_psum.tile([P, PACK, MAPS], F32, name="occ_acc")
            for t in range(PACK):
                nc.tensor.matmul(
                    out=acc[:, t, :],
                    lhsT=occ_hidden[n][:, t * P : (t + 1) * P],
                    rhs=w_occ_t[:],
                    start=True,
                    stop=True,
                )
            occ_acc[n] = acc

        def occ_abs(n):
            if n % 2 == 0:
                occ_grouped[n] = work.tile([P, 2, MAPS, PACK], BF16, name="occ_grouped", align_bytes=64)
                occ_grouped[n + 1] = occ_grouped[n]
            nc.scalar.activation(
                out=occ_grouped[n][:, n % 2, :, :],
                in_=occ_acc[n][:].rearrange("p t o -> p o t"),
                func=mybir.ActivationFunctionType.Abs,
            )

        def occ_due(n):
            if n >= ROUNDS - 2:
                return [n]
            return [n - 1, n] if n % 2 == 1 else []

        def quantise_occ(n):
            rounds = occ_due(n)
            if not rounds:
                return
            first = rounds[0] % 2
            count = len(rounds)
            codes = codes_pool.tile([P, count, MAPS], U32, name="occ_codes", align_bytes=64)
            scales = codes_pool.tile([P, count, MAPS], U8, name="occ_scales", align_bytes=64)
            nc.vector.quantize_mx(
                out=codes[:].rearrange("p r o -> p (r o)").bitcast(FP8X4),
                scales=scales[:].rearrange("p r o -> p (r o)"),
                in_=occ_grouped[n][:, first : first + count, :, :].rearrange("p r o t -> p (r o t)"),
            )
            for i, m in enumerate(rounds):
                occ_codes[m] = codes[:, i, :]
                occ_scales[m] = scales[:, i, :]

        def parts(b):
            return LAST_PARTS if b == SAMPLES - 1 else ((0, C_IN),)

        def second_product(n):
            b, r = divmod(n, ROUNDS_PER_SAMPLE)
            ranges = parts(b)
            if n == ROUNDS - 1:
                for m in range(n - r, n):
                    sum_up(m, b, len(ranges) - 1)
            for i in range(len(ranges)):
                if b < SAMPLES - 1 or i < len(ranges) - 1 or n == ROUNDS - 1:
                    sum_up(n, b, i)

        def sum_up(n, b, i):
                r = n % ROUNDS_PER_SAMPLE
                lo, hi = parts(b)[i]
                if r == 0:
                    late = b == SAMPLES - 1 and i == len(parts(b)) - 1
                    pool = feat_psum if late else out_psum
                    out_acc[(b, i)] = pool.tile(
                        [MAPS, hi - lo], F32, name="out_acc", tag="feat_acc" if late else "out_acc"
                    )
                channels = slice(lo, hi)
                nc.tensor.matmul_mx(
                    out=out_acc[(b, i)][:],
                    lhsT=occ_codes[n].bitcast(FP8X4),
                    lhsT_scale=occ_scales[n],
                    rhs=feat_codes[n][:, channels].bitcast(FP8X4),
                    rhs_scale=feat_scales[n][:, channels],
                    start=(r == 0),
                    stop=(r == ROUNDS_PER_SAMPLE - 1),
                )

        def store_sample(b):
            for i, (lo, hi) in enumerate(parts(b)):
                mean = work.tile([MAPS, hi - lo], F32, name="mean")
                nc.scalar.mul(out=mean[:], in_=out_acc[(b, i)][:], mul=1.0 / VOXELS)
                nc.sync.dma_start(out=out[b, :, lo:hi], in_=mean[:])

        def exists(n):
            return 0 <= n < ROUNDS

        def vector_blocks(n):
            first_tail_round = ROUNDS - TAIL_ROUNDS
            if n >= first_tail_round:
                return C_BLOCKS - TAIL_BLOCKS[n - first_tail_round]
            if n >= SCALAR_FIRST and (n - SCALAR_FIRST) % SCALAR_EVERY == 0:
                return C_BLOCKS - 1
            return C_BLOCKS

        def scalar_blocks(n):
            return list(range(vector_blocks(n), C_BLOCKS)) if exists(n) else []

        regroup(0, 0)
        for n in range(-2, ROUNDS):
            lead = 2 if n == 0 else 0
            for cb in range(lead):
                add_bias(n, cb)
            if exists(n + 1):
                feat_grouped[n + 1] = work.tile(
                    [P, C_IN, PACK], BF16, name="feat_grouped", align_bytes=64
                )
                if n == 2:
                    vector_regroup()
                quantise_h(n + 1)
                if n == -1:
                    nc.vector.tensor_copy(out=bias[:], in_=bias_acc[:])
                    nc.vector.tensor_copy(out=w_occ_t[:], in_=w_occ_acc[:])
                for cb in scalar_blocks(n + 1):
                    rows_product(n + 1, cb)
                for cb in range(lead + 1):
                    first_product(n + 1, cb)
                if n < 0:
                    occ_product(n + 1)
            if exists(n + 2):
                regroup(n + 2, 1)
            for cb in scalar_blocks(n):
                regroup_rows(n, cb)
            if n == SCALAR_FIRST - 2:
                copy_bias_columns()
            if exists(n + 1):
                occ_abs(n + 1)
            if exists(n + 3):
                regroup(n + 3, 0)
            for cb in scalar_blocks(n + 1):
                add_bias_rows(n + 1, cb)
            if n > 0 and n % ROUNDS_PER_SAMPLE == 0:
                store_sample(n // ROUNDS_PER_SAMPLE - 1)
            for cb in range(lead, C_BLOCKS):
                if exists(n) and cb < vector_blocks(n):
                    add_bias(n, cb)
                if exists(n + 1) and cb + 1 < vector_blocks(n + 1):
                    first_product(n + 1, cb + 1)
            for cb in scalar_blocks(n + 1):
                turn_rows(n + 1, cb)
            if exists(n):
                quantise_feat(n)
                for m in occ_due(n):
                    second_product(m)
            if n >= -1 and exists(n + 2):
                occ_product(n + 2)
            if n == SCALAR_FIRST - 3:
                turn_bias()
            if n == ROUNDS - 1:
                store_sample(SAMPLES - 1)
            if exists(n + 2 + ROUNDS_IN_FLIGHT):
                load_round(n + 2 + ROUNDS_IN_FLIGHT)
